import numpy as np
import ml_dtypes


def mxq(x, axis, fmt="e4m3"):
    dtype, down = {"e4m3": (ml_dtypes.float8_e4m3fn, 7), "e5m2": (ml_dtypes.float8_e5m2, 14)}[fmt]
    v = np.moveaxis(np.asarray(x, np.float32).astype(ml_dtypes.bfloat16).astype(np.float64), axis, -1)
    blocks = v.reshape(v.shape[:-1] + (-1, 32))
    amax = np.abs(blocks).max(-1, keepdims=True)
    byte = np.maximum(np.where(amax > 0, np.frexp(amax)[1] - 1 + 127, 0) - down, 1)
    scale = np.exp2(byte - 127.0)
    codes = (blocks / scale).astype(np.float32).astype(dtype).astype(np.float64)
    return np.moveaxis((codes * scale).reshape(v.shape), -1, axis)


WIDE = False


def mx_kscale(k):
    if not WIDE:
        return np.ones(k)
    levels = np.array([10, -10, 5, -5, 0])
    if k % 512:
        return np.exp2(np.random.permutation(np.resize(levels, k // 32))).repeat(32)
    a = np.empty((k // 512, 16))
    for p in range(k // 512):
        a[p, :8] = np.random.permutation(np.resize(levels, 8))
        for g in range(8):
            far = levels[np.abs(levels - a[p, g]) >= 10]
            a[p, g + 8] = far[np.random.randint(len(far))]
    return np.exp2(a.ravel()).repeat(32)


BF16 = ml_dtypes.bfloat16


def bf(x):
    return np.asarray(x, np.float32).astype(BF16)


def f64(x):
    return np.asarray(x).astype(np.float64)


B, T, E, H, DK, C = 1, 1024, 1024, 4, 256, 512
DV = 2 * DK
F = H * DV
EPS = 1e-5


def setup_inputs():
    s, t = mx_kscale(E), mx_kscale(F)
    o = np.random.standard_normal((B, T, H, DV)) * 5.0 * np.exp(0.5 * np.random.standard_normal((B, T, H, 1)))
    return {"o_ret": bf(o),
            "x": bf(np.random.standard_normal((B, T, E)) * s),
            "Wg": bf(np.random.standard_normal((E, F)) / np.sqrt(E) / s[:, None] * t),
            "gn_weight": bf(1.0 + 0.1 * np.random.standard_normal(DV)),
            "Wo": bf(np.random.standard_normal((F, E)) / np.sqrt(F) / t[:, None])}


def reference(o_ret, x, Wg, gn_weight, Wo):
    o = f64(o_ret)
    rms = np.sqrt(np.mean(o * o, axis=-1, keepdims=True) + EPS)
    o = o / rms * f64(gn_weight)
    g = mxq(f64(x), 2, "e4m3") @ mxq(f64(Wg), 0, "e4m3")
    h = o.reshape(B, T, F) * g
    return mxq(h, 2, "e4m3") @ mxq(f64(Wo), 0, "e4m3")

@@ -1,0 +1,277 @@
+import concourse.mybir as mybir
+from concourse.masks import make_identity
+
+FP8X4 = mybir.dt.float8_e4m3fn_x4
+BF16 = mybir.dt.bfloat16
+F32 = mybir.dt.float32
+U32 = mybir.dt.uint32
+U8 = mybir.dt.uint8
+ACT = mybir.ActivationFunctionType
+ALU = mybir.AluOpType
+
+P = 128
+PACK = 4
+K_PASS = P * PACK
+T = 1024
+E = 1024
+HEADS = 4
+DV = 512
+F = HEADS * DV
+N_OUT = 1024
+N_TILE = 512
+T_TILES = T // P
+E_PASSES = E // K_PASS
+N_HALVES = N_OUT // N_TILE
+EPS = 1e-5
+
+FLOPS = 2 * T * E * F + 2 * T * F * N_OUT
+
+
+def tile_multiscaleretention_pc_kernel(tc, o_ret, x, Wg, gn_weight, Wo, out):
+    nc = tc.nc
+    x_view = x.flatten_outer_dims().rearrange("(p i) e -> p i e", i=T_TILES)
+    o_view = o_ret.rearrange("b t h d -> (b t) (h d)").rearrange("(p i) f -> p i f", i=T_TILES)
+    out_view = out.flatten_outer_dims().rearrange("(p i) n -> p i n", i=T_TILES)
+
+    with tc.tile_pool(name="keep", bufs=1) as keep, tc.tile_pool(name="w_stage", bufs=4) as w_stage, tc.tile_pool(
+        name="h0_pool", bufs=2 * HEADS
+    ) as h0_pool, tc.tile_pool(name="pair", bufs=2) as pair, tc.psum_pool(name="psum_g", bufs=2) as psum_g, tc.psum_pool(
+        name="psum_ht", bufs=3
+    ) as psum_ht, tc.psum_pool(name="psum_xt", bufs=1) as psum_xt, tc.psum_pool(
+        name="psum_acc", bufs=2
+    ) as psum_acc:
+        ident = keep.tile([P, P], F32)
+        make_identity(nc, ident[:])
+        eps_col = keep.tile([P, 1], F32)
+        nc.vector.memset(eps_col[:], EPS)
+        gn_cols = keep.tile([P, PACK], BF16)
+        warm = keep.tile([P, 1], F32)
+        nc.scalar.activation(out=warm[:], in_=eps_col[:], func=ACT.Abs_reciprocal_sqrt)
+
+        x_raw = keep.tile([P, T_TILES, E], BF16)
+        wg_raw = keep.tile([P, E_PASSES, PACK, F], BF16)
+        o_raw = keep.tile([P, T_TILES, F], BF16)
+        wo_raw = keep.tile([P, HEADS, PACK, N_OUT], BF16)
+
+        def load_x(i):
+            nc.sync.dma_start(out=x_raw[:, i, :], in_=x_view[:, i, :])
+
+        def load_o(i):
+            nc.sync.dma_start(out=o_raw[:, i, :], in_=o_view[:, i, :])
+
+        def load_wg(head_pair):
+            cols = slice(2 * DV * head_pair, 2 * DV * (head_pair + 1))
+            for c in range(E_PASSES):
+                nc.sync.dma_start(
+                    out=wg_raw[:, c, :, cols],
+                    in_=Wg[K_PASS * c : K_PASS * (c + 1), cols].rearrange("(p j) f -> p j f", j=PACK),
+                )
+
+        def load_wo(head):
+            nc.sync.dma_start(
+                out=wo_raw[:, head, :, :],
+                in_=Wo[K_PASS * head : K_PASS * (head + 1), :].rearrange("(p j) n -> p j n", j=PACK),
+            )
+
+        load_x(0)
+        nc.sync.dma_start(out=gn_cols[:], in_=gn_weight.rearrange("(p j) -> p j", j=PACK))
+        load_o(0)
+        load_x(1)
+        load_wg(0)
+        load_wg(1)
+        load_o(1)
+        load_wo(0)
+        load_wo(1)
+        load_x(2)
+        load_o(2)
+        load_wo(2)
+        load_wo(3)
+        for i in range(3, T_TILES):
+            load_x(i)
+            load_o(i)
+
+        x_words = x_raw[:].bitcast(F32)
+        x_codes = keep.tile([P, T_TILES, E_PASSES, P], U32, align_bytes=64)
+        x_scales = keep.tile([P, T_TILES, E_PASSES, P], U8, align_bytes=64)
+        x_grouped = {}
+        rinv = {}
+
+        def transpose_x_and_norm(i):
+            xt = psum_xt.tile([P, PACK, P], F32, tag="xt")
+            for c in range(E_PASSES):
+                for u in range(2):
+                    nc.tensor.transpose(
+                        xt[:, 2 * c + u, :], x_words[:, i, 2 * P * c + u : 2 * P * (c + 1) : 2], ident[:]
+                    )
+            grouped = pair.tile([P, E_PASSES, P, PACK], BF16, align_bytes=64, tag="x_grouped")
+            copy = nc.vector.tensor_copy if i < 2 else nc.scalar.copy
+            copy(out=grouped[:].bitcast(F32), in_=xt[:].rearrange("p (c u) t -> p c t u", u=2))
+            x_grouped[i] = grouped
+            ssq = keep.tile([P, HEADS], F32, name="ssq%d" % i)
+            for head in range(HEADS):
+                squares = pair.tile([P, DV], BF16, tag="squares")
+                nc.scalar.activation(
+                    out=squares[:],
+                    in_=o_raw[:, i, DV * head : DV * (head + 1)],
+                    func=ACT.Square,
+                    accum_out=ssq[:, head : head + 1],
+                )
+            rinv[i] = keep.tile([P, HEADS], F32, name="rinv%d" % i)
+            nc.scalar.activation(
+                out=rinv[i][:], in_=ssq[:], func=ACT.Abs_reciprocal_sqrt, scale=1.0 / DV, bias=eps_col[:]
+            )
+
+        def quantise_x(i):
+            nc.vector.quantize_mx(
+                out=x_codes[:, i, :, :].rearrange("p c t -> p (c t)").bitcast(FP8X4),
+                scales=x_scales[:, i, :, :].rearrange("p c t -> p (c t)"),
+                in_=x_grouped[i][:].rearrange("p c t j -> p (c t j)"),
+            )
+
+        wg_codes = keep.tile([P, E_PASSES, F], U32, align_bytes=64)
+        wg_scales = keep.tile([P, E_PASSES, F], U8, align_bytes=64)
+        wo_codes = keep.tile([P, HEADS, N_OUT], U32, align_bytes=64)
+        wo_scales = keep.tile([P, HEADS, N_OUT], U8, align_bytes=64)
+
+        def regroup(copy, rows):
+            grouped = w_stage.tile([P, N_TILE, PACK], BF16, align_bytes=64, tag="w_grouped")
+            copy(
+                out=grouped[:].rearrange("p (c i) j -> p c j i", i=4),
+                in_=rows.rearrange("p j (c i) -> p c j i", i=4),
+            )
+            return grouped
+
+        def quantise_weights(grouped, codes, scales):
+            nc.vector.quantize_mx(
+                out=codes.bitcast(FP8X4), scales=scales, in_=grouped[:].rearrange("p w j -> p (w j)")
+            )
+
+        def prepare_wg(head_pair):
+            even, odd = 2 * head_pair, 2 * head_pair + 1
+            for c in range(E_PASSES):
+                on_vector = regroup(nc.vector.tensor_copy, wg_raw[:, c, :, DV * even : DV * (even + 1)])
+                on_scalar = regroup(nc.scalar.copy, wg_raw[:, c, :, DV * odd : DV * (odd + 1)])
+                for head, grouped in ((even, on_vector), (odd, on_scalar)):
+                    cols = slice(DV * head, DV * (head + 1))
+                    quantise_weights(grouped, wg_codes[:, c, cols], wg_scales[:, c, cols])
+
+        wo_grouped = {}
+
+        def regroup_wo_on_scalar(head):
+            wo_grouped[(head, 0)] = regroup(nc.scalar.copy, wo_raw[:, head, :, 0:N_TILE])
+
+        def regroup_wo_on_vector(head):
+            wo_grouped[(head, 1)] = regroup(nc.vector.tensor_copy, wo_raw[:, head, :, N_TILE:N_OUT])
+
+        def quantise_wo(head):
+            for half in range(N_HALVES):
+                cols = slice(N_TILE * half, N_TILE * (half + 1))
+                quantise_weights(wo_grouped[(head, half)], wo_codes[:, head, cols], wo_scales[:, head, cols])
+
+        h_codes = keep.tile([P, T_TILES, HEADS, P], U32, align_bytes=64)
+        h_scales = keep.tile([P, T_TILES, HEADS, P], U8, align_bytes=64)
+        g_banks = {}
+        h0_tiles = {}
+        ht_banks = {}
+
+        def gate_matmul(i, head):
+            cols = slice(DV * head, DV * (head + 1))
+            g = psum_g.tile([P, DV], F32, tag="g")
+            for c in range(E_PASSES):
+                nc.tensor.matmul_mx(
+                    out=g[:],
+                    lhsT=x_codes[:, i, c, :].bitcast(FP8X4),
+                    lhsT_scale=x_scales[:, i, c, :],
+                    rhs=wg_codes[:, c, cols].bitcast(FP8X4),
+                    rhs_scale=wg_scales[:, c, cols],
+                    start=(c == 0),
+                    stop=(c == E_PASSES - 1),
+                )
+            g_banks[(i, head)] = g
+
+        def gate_times_norm(i, head):
+            h0 = h0_pool.tile([P, PACK, P], F32, tag="h0")
+            nc.vector.scalar_tensor_tensor(
+                out=h0[:],
+                in0=g_banks[(i, head)][:].rearrange("t (p j) -> t j p", j=PACK),
+                scalar=rinv[i][:, head : head + 1],
+                in1=o_raw[:, i, DV * head : DV * (head + 1)].rearrange("t (p j) -> t j p", j=PACK),
+                op0=ALU.mult,
+                op1=ALU.mult,
+            )
+            h0_tiles[(i, head)] = h0
+
+        def transpose_h(i, head):
+            ht = psum_ht.tile([P, PACK, P], F32, tag="ht")
+            for j in range(PACK):
+                nc.tensor.transpose(ht[:, j, :], h0_tiles[(i, head)][:, j, :], ident[:])
+            ht_banks[(i, head)] = ht
+
+        def weigh_and_quantise_h(i):
+            h_grouped = pair.tile([P, HEADS, P, PACK], BF16, align_bytes=64, tag="h_grouped")
+            for head in range(HEADS):
+                nc.vector.tensor_tensor(
+                    out=h_grouped[:, head, :, :],
+                    in0=ht_banks[(i, head)][:].rearrange("p j t -> p t j"),
+                    in1=gn_cols[:].unsqueeze(1).to_broadcast([P, P, PACK]),
+                    op=ALU.mult,
+                )
+            nc.vector.quantize_mx(
+                out=h_codes[:, i, :, :].rearrange("p h t -> p (h t)").bitcast(FP8X4),
+                scales=h_scales[:, i, :, :].rearrange("p h t -> p (h t)"),
+                in_=h_grouped[:].rearrange("p h t j -> p (h t j)"),
+            )
+
+        def project_and_store(i):
+            acc = [psum_acc.tile([P, N_TILE], F32, name="acc%d" % half, tag="acc") for half in range(N_HALVES)]
+            for head in range(HEADS):
+                for half in range(N_HALVES):
+                    cols = slice(N_TILE * half, N_TILE * (half + 1))
+                    nc.tensor.matmul_mx(
+                        out=acc[half][:],
+                        lhsT=h_codes[:, i, head, :].bitcast(FP8X4),
+                        lhsT_scale=h_scales[:, i, head, :],
+                        rhs=wo_codes[:, head, cols].bitcast(FP8X4),
+                        rhs_scale=wo_scales[:, head, cols],
+                        start=(head == 0),
+                        stop=(head == HEADS - 1),
+                    )
+            result = pair.tile([P, N_OUT], F32, tag="result")
+            for half in range(N_HALVES):
+                nc.scalar.copy(out=result[:, N_TILE * half : N_TILE * (half + 1)], in_=acc[half][:])
+            nc.sync.dma_start(out=out_view[:, i, :], in_=result[:])
+
+        transpose_x_and_norm(0)
+        quantise_x(0)
+        prepare_wg(0)
+        prepare_wg(1)
+
+        for step in range(T_TILES + 2):
+            if step + 1 < T_TILES:
+                transpose_x_and_norm(step + 1)
+            if step < 2:
+                regroup_wo_on_scalar(2 * step)
+                regroup_wo_on_scalar(2 * step + 1)
+            if 1 <= step <= T_TILES:
+                for head in range(HEADS):
+                    transpose_h(step - 1, head)
+            if step < T_TILES:
+                gate_matmul(step, 0)
+                gate_matmul(step, 1)
+            if step >= 2:
+                project_and_store(step - 2)
+            if step < T_TILES:
+                gate_matmul(step, 2)
+                gate_matmul(step, 3)
+            if 1 <= step <= T_TILES:
+                weigh_and_quantise_h(step - 1)
+            if step + 1 < T_TILES:
+                quantise_x(step + 1)
+            if step < T_TILES:
+                for head in range(HEADS):
+                    gate_times_norm(step, head)
+            if step < 2:
+                regroup_wo_on_vector(2 * step)
+                regroup_wo_on_vector(2 * step + 1)
+                quantise_wo(2 * step)
+                quantise_wo(2 * step + 1)

@@ -23,6 +23,7 @@ T_TILES = T // P
 E_PASSES = E // K_PASS
 N_HALVES = N_OUT // N_TILE
 EPS = 1e-5
+OG_TILES = 4
 
 FLOPS = 2 * T * E * F + 2 * T * F * N_OUT
 
@@ -34,27 +35,32 @@ def tile_multiscaleretention_pc_kernel(tc, o_ret, x, Wg, gn_weight, Wo, out):
     out_view = out.flatten_outer_dims().rearrange("(p i) n -> p i n", i=T_TILES)
 
     with tc.tile_pool(name="keep", bufs=1) as keep, tc.tile_pool(name="w_stage", bufs=4) as w_stage, tc.tile_pool(
-        name="h0_pool", bufs=2 * HEADS
-    ) as h0_pool, tc.tile_pool(name="pair", bufs=2) as pair, tc.psum_pool(name="psum_g", bufs=2) as psum_g, tc.psum_pool(
-        name="psum_ht", bufs=3
+        name="w_raw", bufs=5
+    ) as w_raw, tc.tile_pool(name="x_pool", bufs=4) as x_pool, tc.tile_pool(
+        name="og_pool", bufs=OG_TILES * HEADS
+    ) as og_pool, tc.tile_pool(name="hb_pool", bufs=2 * HEADS) as hb_pool, tc.tile_pool(name="pair", bufs=2) as pair, tc.psum_pool(name="psum_g", bufs=3) as psum_g, tc.psum_pool(
+        name="psum_ht", bufs=2
     ) as psum_ht, tc.psum_pool(name="psum_xt", bufs=1) as psum_xt, tc.psum_pool(
         name="psum_acc", bufs=2
     ) as psum_acc:
+        gn_cols = keep.tile([P, PACK], BF16)
         ident = keep.tile([P, P], F32)
         make_identity(nc, ident[:])
+        ident_bf16 = keep.tile([P, P], BF16)
+        make_identity(nc, ident_bf16[:])
         eps_col = keep.tile([P, 1], F32)
         nc.vector.memset(eps_col[:], EPS)
-        gn_cols = keep.tile([P, PACK], BF16)
         warm = keep.tile([P, 1], F32)
         nc.scalar.activation(out=warm[:], in_=eps_col[:], func=ACT.Abs_reciprocal_sqrt)
 
-        x_raw = keep.tile([P, T_TILES, E], BF16)
-        wg_raw = keep.tile([P, E_PASSES, PACK, F], BF16)
+        x_raw = {}
+        wg_raw = {}
         o_raw = keep.tile([P, T_TILES, F], BF16)
-        wo_raw = keep.tile([P, HEADS, PACK, N_OUT], BF16)
+        wo_raw = {}
 
         def load_x(i):
-            nc.sync.dma_start(out=x_raw[:, i, :], in_=x_view[:, i, :])
+            x_raw[i] = x_pool.tile([P, E], BF16, name="x_raw", tag="x_raw")
+            nc.sync.dma_start(out=x_raw[i][:], in_=x_view[:, i, :])
 
         def load_o(i):
             nc.sync.dma_start(out=o_raw[:, i, :], in_=o_view[:, i, :])
@@ -62,35 +68,51 @@ def tile_multiscaleretention_pc_kernel(tc, o_ret, x, Wg, gn_weight, Wo, out):
         def load_wg(head_pair):
             cols = slice(2 * DV * head_pair, 2 * DV * (head_pair + 1))
             for c in range(E_PASSES):
+                wg_raw[(c, head_pair)] = w_raw.tile([P, PACK, 2 * DV], BF16, name="wg_raw", tag="w_raw")
                 nc.sync.dma_start(
-                    out=wg_raw[:, c, :, cols],
+                    out=wg_raw[(c, head_pair)][:],
                     in_=Wg[K_PASS * c : K_PASS * (c + 1), cols].rearrange("(p j) f -> p j f", j=PACK),
                 )
 
         def load_wo(head):
+            wo_raw[head] = w_raw.tile([P, PACK, N_OUT], BF16, name="wo_raw", tag="w_raw")
             nc.sync.dma_start(
-                out=wo_raw[:, head, :, :],
+                out=wo_raw[head][:],
                 in_=Wo[K_PASS * head : K_PASS * (head + 1), :].rearrange("(p j) n -> p j n", j=PACK),
             )
 
         load_x(0)
         nc.sync.dma_start(out=gn_cols[:], in_=gn_weight.rearrange("(p j) -> p j", j=PACK))
         load_o(0)
-        load_x(1)
         load_wg(0)
-        load_wg(1)
+        load_x(1)
         load_o(1)
+        load_wg(1)
+        load_o(2)
+        load_x(2)
         load_wo(0)
         load_wo(1)
-        load_x(2)
-        load_o(2)
         load_wo(2)
         load_wo(3)
         for i in range(3, T_TILES):
             load_x(i)
             load_o(i)
 
-        x_words = x_raw[:].bitcast(F32)
+        def in_word_order(features):
+            return features.rearrange("t (p u e) -> t u p e", u=2, e=2)
+
+        gn_bank = psum_xt.tile([P, PACK, P], F32, tag="xt")
+        for j in range(PACK):
+            nc.tensor.matmul(
+                out=gn_bank[:, j, :],
+                lhsT=gn_cols[:, j : j + 1].to_broadcast([P, P]),
+                rhs=ident_bf16[:],
+                start=True,
+                stop=True,
+            )
+        gn_all = keep.tile([P, 2, P, 2], F32)
+        nc.vector.tensor_copy(out=gn_all[:], in_=gn_bank[:].rearrange("t (u e) p -> t u p e", e=2))
+
         x_codes = keep.tile([P, T_TILES, E_PASSES, P], U32, align_bytes=64)
         x_scales = keep.tile([P, T_TILES, E_PASSES, P], U8, align_bytes=64)
         x_grouped = {}
@@ -98,10 +120,11 @@ def tile_multiscaleretention_pc_kernel(tc, o_ret, x, Wg, gn_weight, Wo, out):
 
         def transpose_x_and_norm(i):
             xt = psum_xt.tile([P, PACK, P], F32, tag="xt")
+            x_words = x_raw[i][:].bitcast(F32)
             for c in range(E_PASSES):
                 for u in range(2):
                     nc.tensor.transpose(
-                        xt[:, 2 * c + u, :], x_words[:, i, 2 * P * c + u : 2 * P * (c + 1) : 2], ident[:]
+                        xt[:, 2 * c + u, :], x_words[:, 2 * P * c + u : 2 * P * (c + 1) : 2], ident[:]
                     )
             grouped = pair.tile([P, E_PASSES, P, PACK], BF16, align_bytes=64, tag="x_grouped")
             copy = nc.vector.tensor_copy if i < 2 else nc.scalar.copy
@@ -141,6 +164,14 @@ def tile_multiscaleretention_pc_kernel(tc, o_ret, x, Wg, gn_weight, Wo, out):
             )
             return grouped
 
+        def regroup_in_word_order(copy, rows):
+            grouped = w_stage.tile([P, N_TILE, PACK], BF16, align_bytes=64, tag="w_grouped")
+            copy(
+                out=grouped[:].rearrange("p (u c e) j -> p c j u e", u=2, e=2),
+                in_=rows.rearrange("p j (c u e) -> p c j u e", u=2, e=2),
+            )
+            return grouped
+
         def quantise_weights(grouped, codes, scales):
             nc.vector.quantize_mx(
                 out=codes.bitcast(FP8X4), scales=scales, in_=grouped[:].rearrange("p w j -> p (w j)")
@@ -149,8 +180,8 @@ def tile_multiscaleretention_pc_kernel(tc, o_ret, x, Wg, gn_weight, Wo, out):
         def prepare_wg(head_pair):
             even, odd = 2 * head_pair, 2 * head_pair + 1
             for c in range(E_PASSES):
-                on_vector = regroup(nc.vector.tensor_copy, wg_raw[:, c, :, DV * even : DV * (even + 1)])
-                on_scalar = regroup(nc.scalar.copy, wg_raw[:, c, :, DV * odd : DV * (odd + 1)])
+                on_vector = regroup_in_word_order(nc.vector.tensor_copy, wg_raw[(c, head_pair)][:, :, 0:DV])
+                on_scalar = regroup_in_word_order(nc.scalar.copy, wg_raw[(c, head_pair)][:, :, DV : 2 * DV])
                 for head, grouped in ((even, on_vector), (odd, on_scalar)):
                     cols = slice(DV * head, DV * (head + 1))
                     quantise_weights(grouped, wg_codes[:, c, cols], wg_scales[:, c, cols])
@@ -158,10 +189,10 @@ def tile_multiscaleretention_pc_kernel(tc, o_ret, x, Wg, gn_weight, Wo, out):
         wo_grouped = {}
 
         def regroup_wo_on_scalar(head):
-            wo_grouped[(head, 0)] = regroup(nc.scalar.copy, wo_raw[:, head, :, 0:N_TILE])
+            wo_grouped[(head, 0)] = regroup(nc.scalar.copy, wo_raw[head][:, :, 0:N_TILE])
 
         def regroup_wo_on_vector(head):
-            wo_grouped[(head, 1)] = regroup(nc.vector.tensor_copy, wo_raw[:, head, :, N_TILE:N_OUT])
+            wo_grouped[(head, 1)] = regroup(nc.vector.tensor_copy, wo_raw[head][:, :, N_TILE:N_OUT])
 
         def quantise_wo(head):
             for half in range(N_HALVES):
@@ -172,7 +203,21 @@ def tile_multiscaleretention_pc_kernel(tc, o_ret, x, Wg, gn_weight, Wo, out):
         h_scales = keep.tile([P, T_TILES, HEADS, P], U8, align_bytes=64)
         g_banks = {}
         h0_tiles = {}
+        og_tiles = {}
+        h_grouped_tiles = {}
         ht_banks = {}
+
+        def weigh_o(i):
+            for head in range(HEADS):
+                og = og_pool.tile([P, 2, P, 2], F32, tag="og")
+                nc.vector.tensor_tensor(
+                    out=og[:],
+                    in0=in_word_order(o_raw[:, i, DV * head : DV * (head + 1)]),
+                    in1=gn_all[:],
+                    op=ALU.mult,
+                )
+                og_tiles[(i, head)] = og
+
 
         def gate_matmul(i, head):
             cols = slice(DV * head, DV * (head + 1))
@@ -189,37 +234,40 @@ def tile_multiscaleretention_pc_kernel(tc, o_ret, x, Wg, gn_weight, Wo, out):
                 )
             g_banks[(i, head)] = g
 
-        def gate_times_norm(i, head):
-            h0 = h0_pool.tile([P, PACK, P], F32, tag="h0")
+        def gate_times_weighed_norm(i, head):
+            h0 = hb_pool.tile([P, DV], BF16, tag="hb")
             nc.vector.scalar_tensor_tensor(
                 out=h0[:],
-                in0=g_banks[(i, head)][:].rearrange("t (p j) -> t j p", j=PACK),
+                in0=g_banks[(i, head)][:],
                 scalar=rinv[i][:, head : head + 1],
-                in1=o_raw[:, i, DV * head : DV * (head + 1)].rearrange("t (p j) -> t j p", j=PACK),
+                in1=og_tiles[(i, head)][:].rearrange("t u p e -> t (u p e)"),
                 op0=ALU.mult,
                 op1=ALU.mult,
             )
             h0_tiles[(i, head)] = h0
 
-        def transpose_h(i, head):
-            ht = psum_ht.tile([P, PACK, P], F32, tag="ht")
-            for j in range(PACK):
-                nc.tensor.transpose(ht[:, j, :], h0_tiles[(i, head)][:, j, :], ident[:])
-            ht_banks[(i, head)] = ht
+        def transpose_h_words(i):
+            h_grouped_tiles[i] = pair.tile([P, HEADS, P, PACK], BF16, align_bytes=64, tag="h_grouped", name="h_grouped")
+            for pair_of_heads in range(2):
+                ht = psum_ht.tile([P, PACK, P], F32, tag="ht")
+                for hu in range(PACK):
+                    words = h0_tiles[(i, 2 * pair_of_heads + hu // 2)][:].bitcast(F32)
+                    u = hu % 2
+                    nc.tensor.transpose(ht[:, hu, :], words[:, P * u : P * (u + 1)], ident[:])
+                ht_banks[(i, pair_of_heads)] = ht
 
-        def weigh_and_quantise_h(i):
-            h_grouped = pair.tile([P, HEADS, P, PACK], BF16, align_bytes=64, tag="h_grouped")
-            for head in range(HEADS):
-                nc.vector.tensor_tensor(
-                    out=h_grouped[:, head, :, :],
-                    in0=ht_banks[(i, head)][:].rearrange("p j t -> p t j"),
-                    in1=gn_cols[:].unsqueeze(1).to_broadcast([P, P, PACK]),
-                    op=ALU.mult,
+        def copy_h_words(i):
+            for pair_of_heads in range(2):
+                nc.scalar.copy(
+                    out=h_grouped_tiles[i][:, 2 * pair_of_heads : 2 * pair_of_heads + 2, :, :].bitcast(F32),
+                    in_=ht_banks[(i, pair_of_heads)][:].rearrange("p (h u) t -> p h t u", u=2),
                 )
+
+        def quantise_h(i):
             nc.vector.quantize_mx(
                 out=h_codes[:, i, :, :].rearrange("p h t -> p (h t)").bitcast(FP8X4),
                 scales=h_scales[:, i, :, :].rearrange("p h t -> p (h t)"),
-                in_=h_grouped[:].rearrange("p h t j -> p (h t j)"),
+                in_=h_grouped_tiles[i][:].rearrange("p h t j -> p (h t j)"),
             )
 
         def project_and_store(i):
@@ -243,35 +291,48 @@ def tile_multiscaleretention_pc_kernel(tc, o_ret, x, Wg, gn_weight, Wo, out):
 
         transpose_x_and_norm(0)
         quantise_x(0)
+        weigh_o(0)
         prepare_wg(0)
+        gate_matmul(0, 0)
+        gate_matmul(0, 1)
+        transpose_x_and_norm(1)
+        gate_times_weighed_norm(0, 0)
+        gate_times_weighed_norm(0, 1)
         prepare_wg(1)
+        gate_matmul(0, 2)
+        gate_matmul(0, 3)
+        quantise_x(1)
+        gate_times_weighed_norm(0, 2)
+        gate_times_weighed_norm(0, 3)
+        weigh_o(1)
 
-        for step in range(T_TILES + 2):
+        for step in range(1, T_TILES + 2):
             if step + 1 < T_TILES:
                 transpose_x_and_norm(step + 1)
-            if step < 2:
-                regroup_wo_on_scalar(2 * step)
-                regroup_wo_on_scalar(2 * step + 1)
-            if 1 <= step <= T_TILES:
-                for head in range(HEADS):
-                    transpose_h(step - 1, head)
+            if step <= T_TILES:
+                transpose_h_words(step - 1)
+                copy_h_words(step - 1)
             if step < T_TILES:
                 gate_matmul(step, 0)
                 gate_matmul(step, 1)
+            if step <= 2:
+                regroup_wo_on_scalar(2 * step - 2)
+                regroup_wo_on_scalar(2 * step - 1)
+                regroup_wo_on_vector(2 * step - 2)
+                regroup_wo_on_vector(2 * step - 1)
+                quantise_wo(2 * step - 2)
+                quantise_wo(2 * step - 1)
             if step >= 2:
                 project_and_store(step - 2)
             if step < T_TILES:
                 gate_matmul(step, 2)
                 gate_matmul(step, 3)
-            if 1 <= step <= T_TILES:
-                weigh_and_quantise_h(step - 1)
             if step + 1 < T_TILES:
                 quantise_x(step + 1)
+            if step <= T_TILES:
+                quantise_h(step - 1)
             if step < T_TILES:
                 for head in range(HEADS):
-                    gate_times_norm(step, head)
-            if step < 2:
-                regroup_wo_on_vector(2 * step)
-                regroup_wo_on_vector(2 * step + 1)
-                quantise_wo(2 * step)
-                quantise_wo(2 * step + 1)
+                    gate_times_weighed_norm(step, head)
+                if step + 1 < T_TILES:
+                    weigh_o(step + 1)

@@ -87,9 +87,9 @@ def tile_multiscaleretention_pc_kernel(tc, o_ret, x, Wg, gn_weight, Wo, out):
         load_wg(0)
         load_x(1)
         load_o(1)
+        load_x(2)
         load_wg(1)
         load_o(2)
-        load_x(2)
         load_wo(0)
         load_wo(1)
         load_wo(2)
@@ -101,24 +101,26 @@ def tile_multiscaleretention_pc_kernel(tc, o_ret, x, Wg, gn_weight, Wo, out):
         def in_word_order(features):
             return features.rearrange("t (p u e) -> t u p e", u=2, e=2)
 
-        gn_bank = psum_xt.tile([P, PACK, P], F32, tag="xt")
-        for j in range(PACK):
-            nc.tensor.matmul(
-                out=gn_bank[:, j, :],
-                lhsT=gn_cols[:, j : j + 1].to_broadcast([P, P]),
-                rhs=ident_bf16[:],
-                start=True,
-                stop=True,
-            )
         gn_all = keep.tile([P, 2, P, 2], F32)
-        nc.vector.tensor_copy(out=gn_all[:], in_=gn_bank[:].rearrange("t (u e) p -> t u p e", e=2))
+
+        def spread_gn():
+            gn_bank = psum_xt.tile([P, PACK, P], F32, tag="xt")
+            for j in range(PACK):
+                nc.tensor.matmul(
+                    out=gn_bank[:, j, :],
+                    lhsT=gn_cols[:, j : j + 1].to_broadcast([P, P]),
+                    rhs=ident_bf16[:],
+                    start=True,
+                    stop=True,
+                )
+            nc.vector.tensor_copy(out=gn_all[:], in_=gn_bank[:].rearrange("t (u e) p -> t u p e", e=2))
 
         x_codes = keep.tile([P, T_TILES, E_PASSES, P], U32, align_bytes=64)
         x_scales = keep.tile([P, T_TILES, E_PASSES, P], U8, align_bytes=64)
         x_grouped = {}
         rinv = {}
 
-        def transpose_x_and_norm(i):
+        def transpose_x(i):
             xt = psum_xt.tile([P, PACK, P], F32, tag="xt")
             x_words = x_raw[i][:].bitcast(F32)
             for c in range(E_PASSES):
@@ -127,9 +129,11 @@ def tile_multiscaleretention_pc_kernel(tc, o_ret, x, Wg, gn_weight, Wo, out):
                         xt[:, 2 * c + u, :], x_words[:, 2 * P * c + u : 2 * P * (c + 1) : 2], ident[:]
                     )
             grouped = pair.tile([P, E_PASSES, P, PACK], BF16, align_bytes=64, tag="x_grouped")
-            copy = nc.vector.tensor_copy if i < 2 else nc.scalar.copy
+            copy = nc.vector.tensor_copy if i == 0 else nc.scalar.copy
             copy(out=grouped[:].bitcast(F32), in_=xt[:].rearrange("p (c u) t -> p c t u", u=2))
             x_grouped[i] = grouped
+
+        def square_o(i):
             ssq = keep.tile([P, HEADS], F32, name="ssq%d" % i)
             for head in range(HEADS):
                 squares = pair.tile([P, DV], BF16, tag="squares")
@@ -177,19 +181,22 @@ def tile_multiscaleretention_pc_kernel(tc, o_ret, x, Wg, gn_weight, Wo, out):
                 out=codes.bitcast(FP8X4), scales=scales, in_=grouped[:].rearrange("p w j -> p (w j)")
             )
 
-        def prepare_wg(head_pair):
-            even, odd = 2 * head_pair, 2 * head_pair + 1
-            for c in range(E_PASSES):
-                on_vector = regroup_in_word_order(nc.vector.tensor_copy, wg_raw[(c, head_pair)][:, :, 0:DV])
-                on_scalar = regroup_in_word_order(nc.scalar.copy, wg_raw[(c, head_pair)][:, :, DV : 2 * DV])
-                for head, grouped in ((even, on_vector), (odd, on_scalar)):
-                    cols = slice(DV * head, DV * (head + 1))
-                    quantise_weights(grouped, wg_codes[:, c, cols], wg_scales[:, c, cols])
+        wg_grouped = {}
+
+        def regroup_wg(copy, c, head):
+            first = DV * (head % 2)
+            wg_grouped[(c, head)] = regroup_in_word_order(copy, wg_raw[(c, head // 2)][:, :, first : first + DV])
+
+        def quantise_wg(c, head):
+            cols = slice(DV * head, DV * (head + 1))
+            quantise_weights(wg_grouped[(c, head)], wg_codes[:, c, cols], wg_scales[:, c, cols])
 
         wo_grouped = {}
 
         def regroup_wo_on_scalar(head):
             wo_grouped[(head, 0)] = regroup(nc.scalar.copy, wo_raw[head][:, :, 0:N_TILE])
+            if head % 2 == 1:
+                wo_grouped[(head, 1)] = regroup(nc.scalar.copy, wo_raw[head][:, :, N_TILE:N_OUT])
 
         def regroup_wo_on_vector(head):
             wo_grouped[(head, 1)] = regroup(nc.vector.tensor_copy, wo_raw[head][:, :, N_TILE:N_OUT])
@@ -263,55 +270,93 @@ def tile_multiscaleretention_pc_kernel(tc, o_ret, x, Wg, gn_weight, Wo, out):
                     in_=ht_banks[(i, pair_of_heads)][:].rearrange("p (h u) t -> p h t u", u=2),
                 )
 
-        def quantise_h(i):
+        def quantise_h(i, heads=slice(0, HEADS)):
             nc.vector.quantize_mx(
-                out=h_codes[:, i, :, :].rearrange("p h t -> p (h t)").bitcast(FP8X4),
-                scales=h_scales[:, i, :, :].rearrange("p h t -> p (h t)"),
-                in_=h_grouped_tiles[i][:].rearrange("p h t j -> p (h t j)"),
+                out=h_codes[:, i, heads, :].rearrange("p h t -> p (h t)").bitcast(FP8X4),
+                scales=h_scales[:, i, heads, :].rearrange("p h t -> p (h t)"),
+                in_=h_grouped_tiles[i][:, heads, :, :].rearrange("p h t j -> p (h t j)"),
             )
+
+        def project_head(acc, i, head, half):
+            cols = slice(N_TILE * half, N_TILE * (half + 1))
+            nc.tensor.matmul_mx(
+                out=acc[half][:],
+                lhsT=h_codes[:, i, head, :].bitcast(FP8X4),
+                lhsT_scale=h_scales[:, i, head, :],
+                rhs=wo_codes[:, head, cols].bitcast(FP8X4),
+                rhs_scale=wo_scales[:, head, cols],
+                start=(head == 0),
+                stop=(head == HEADS - 1),
+            )
+
+        def finish_last_tile(i):
+            acc = [psum_acc.tile([P, N_TILE], F32, name="acc%d" % half, tag="acc") for half in range(N_HALVES)]
+            for first in (0, 2):
+                quantise_h(i, slice(first, first + 2))
+            for first in (0, 2):
+                for half in range(N_HALVES):
+                    for head in (first, first + 1):
+                        project_head(acc, i, head, half)
+            for half, copy in enumerate((nc.vector.tensor_copy, nc.scalar.copy)):
+                cols = slice(N_TILE * half, N_TILE * (half + 1))
+                result = pair.tile([P, N_TILE], F32, name="last_result", tag="last_result")
+                copy(out=result[:], in_=acc[half][:])
+                nc.sync.dma_start(out=out_view[:, i, cols], in_=result[:])
 
         def project_and_store(i):
             acc = [psum_acc.tile([P, N_TILE], F32, name="acc%d" % half, tag="acc") for half in range(N_HALVES)]
             for head in range(HEADS):
                 for half in range(N_HALVES):
-                    cols = slice(N_TILE * half, N_TILE * (half + 1))
-                    nc.tensor.matmul_mx(
-                        out=acc[half][:],
-                        lhsT=h_codes[:, i, head, :].bitcast(FP8X4),
-                        lhsT_scale=h_scales[:, i, head, :],
-                        rhs=wo_codes[:, head, cols].bitcast(FP8X4),
-                        rhs_scale=wo_scales[:, head, cols],
-                        start=(head == 0),
-                        stop=(head == HEADS - 1),
-                    )
+                    project_head(acc, i, head, half)
             result = pair.tile([P, N_OUT], F32, tag="result")
             for half in range(N_HALVES):
                 nc.scalar.copy(out=result[:, N_TILE * half : N_TILE * (half + 1)], in_=acc[half][:])
             nc.sync.dma_start(out=out_view[:, i, :], in_=result[:])
 
-        transpose_x_and_norm(0)
-        quantise_x(0)
-        weigh_o(0)
-        prepare_wg(0)
-        gate_matmul(0, 0)
-        gate_matmul(0, 1)
-        transpose_x_and_norm(1)
-        gate_times_weighed_norm(0, 0)
-        gate_times_weighed_norm(0, 1)
-        prepare_wg(1)
-        gate_matmul(0, 2)
-        gate_matmul(0, 3)
-        quantise_x(1)
-        gate_times_weighed_norm(0, 2)
-        gate_times_weighed_norm(0, 3)
-        weigh_o(1)
+        with tc.manual_schedule(engines={mybir.EngineType.PE, mybir.EngineType.DVE, mybir.EngineType.Activation}):
+            spread_gn()
+            transpose_x(0)
+            square_o(0)
+            quantise_x(0)
+            weigh_o(0)
+            for c in range(E_PASSES):
+                regroup_wg(nc.scalar.copy, c, 1)
+            transpose_x(1)
+            regroup_wg(nc.vector.tensor_copy, 0, 0)
+            quantise_wg(0, 0)
+            regroup_wg(nc.vector.tensor_copy, 1, 0)
+            quantise_wg(0, 1)
+            quantise_wg(1, 0)
+            quantise_wg(1, 1)
+            gate_matmul(0, 0)
+            gate_matmul(0, 1)
+            gate_times_weighed_norm(0, 0)
+            quantise_x(1)
+            gate_times_weighed_norm(0, 1)
+            regroup_wg(nc.scalar.copy, 0, 3)
+            square_o(1)
+            transpose_x(2)
+            regroup_wg(nc.scalar.copy, 1, 3)
+            weigh_o(1)
+            regroup_wg(nc.vector.tensor_copy, 0, 2)
+            quantise_wg(0, 2)
+            regroup_wg(nc.vector.tensor_copy, 1, 2)
+            quantise_wg(0, 3)
+            quantise_wg(1, 2)
+            quantise_wg(1, 3)
+            quantise_x(2)
+            gate_matmul(0, 2)
+            gate_matmul(0, 3)
+            gate_times_weighed_norm(0, 2)
+            gate_times_weighed_norm(0, 3)
 
-        for step in range(1, T_TILES + 2):
+        for step in range(1, T_TILES + 1):
+            if step + 2 < T_TILES:
+                transpose_x(step + 2)
             if step + 1 < T_TILES:
-                transpose_x_and_norm(step + 1)
-            if step <= T_TILES:
-                transpose_h_words(step - 1)
-                copy_h_words(step - 1)
+                square_o(step + 1)
+            transpose_h_words(step - 1)
+            copy_h_words(step - 1)
             if step < T_TILES:
                 gate_matmul(step, 0)
                 gate_matmul(step, 1)
@@ -319,7 +364,6 @@ def tile_multiscaleretention_pc_kernel(tc, o_ret, x, Wg, gn_weight, Wo, out):
                 regroup_wo_on_scalar(2 * step - 2)
                 regroup_wo_on_scalar(2 * step - 1)
                 regroup_wo_on_vector(2 * step - 2)
-                regroup_wo_on_vector(2 * step - 1)
                 quantise_wo(2 * step - 2)
                 quantise_wo(2 * step - 1)
             if step >= 2:
@@ -327,10 +371,12 @@ def tile_multiscaleretention_pc_kernel(tc, o_ret, x, Wg, gn_weight, Wo, out):
             if step < T_TILES:
                 gate_matmul(step, 2)
                 gate_matmul(step, 3)
-            if step + 1 < T_TILES:
-                quantise_x(step + 1)
-            if step <= T_TILES:
+            if step + 2 < T_TILES:
+                quantise_x(step + 2)
+            if step < T_TILES:
                 quantise_h(step - 1)
+            else:
+                finish_last_tile(step - 1)
             if step < T_TILES:
                 for head in range(HEADS):
                     gate_times_weighed_norm(step, head)

@@ -217,7 +217,8 @@ def tile_multiscaleretention_pc_kernel(tc, o_ret, x, Wg, gn_weight, Wo, out):
         def weigh_o(i):
             for head in range(HEADS):
                 og = og_pool.tile([P, 2, P, 2], F32, tag="og")
-                nc.vector.tensor_tensor(
+                engine = nc.gpsimd if head == HEADS - 1 and i > 0 else nc.vector
+                engine.tensor_tensor(
                     out=og[:],
                     in0=in_word_order(o_raw[:, i, DV * head : DV * (head + 1)]),
                     in1=gn_all[:],

@@ -38,7 +38,7 @@ def tile_multiscaleretention_pc_kernel(tc, o_ret, x, Wg, gn_weight, Wo, out):
         name="w_raw", bufs=5
     ) as w_raw, tc.tile_pool(name="x_pool", bufs=4) as x_pool, tc.tile_pool(
         name="og_pool", bufs=OG_TILES * HEADS
-    ) as og_pool, tc.tile_pool(name="hb_pool", bufs=2 * HEADS) as hb_pool, tc.tile_pool(name="pair", bufs=2) as pair, tc.psum_pool(name="psum_g", bufs=3) as psum_g, tc.psum_pool(
+    ) as og_pool, tc.tile_pool(name="hb_pool", bufs=2 * HEADS) as hb_pool, tc.tile_pool(name="pair", bufs=2) as pair, tc.tile_pool(name="result_pool", bufs=4) as result_pool, tc.psum_pool(name="psum_g", bufs=3) as psum_g, tc.psum_pool(
         name="psum_ht", bufs=2
     ) as psum_ht, tc.psum_pool(name="psum_xt", bufs=1) as psum_xt, tc.psum_pool(
         name="psum_acc", bufs=2
@@ -74,11 +74,12 @@ def tile_multiscaleretention_pc_kernel(tc, o_ret, x, Wg, gn_weight, Wo, out):
                     in_=Wg[K_PASS * c : K_PASS * (c + 1), cols].rearrange("(p j) f -> p j f", j=PACK),
                 )
 
-        def load_wo(head):
-            wo_raw[head] = w_raw.tile([P, PACK, N_OUT], BF16, name="wo_raw", tag="w_raw")
+        def load_wo(head, half):
+            cols = slice(N_TILE * half, N_TILE * (half + 1))
+            wo_raw[(head, half)] = w_raw.tile([P, PACK, N_TILE], BF16, name="wo_raw", tag="w_raw")
             nc.sync.dma_start(
-                out=wo_raw[head][:],
-                in_=Wo[K_PASS * head : K_PASS * (head + 1), :].rearrange("(p j) n -> p j n", j=PACK),
+                out=wo_raw[(head, half)][:],
+                in_=Wo[K_PASS * head : K_PASS * (head + 1), cols].rearrange("(p j) n -> p j n", j=PACK),
             )
 
         load_x(0)
@@ -90,11 +91,13 @@ def tile_multiscaleretention_pc_kernel(tc, o_ret, x, Wg, gn_weight, Wo, out):
         load_x(2)
         load_wg(1)
         load_o(2)
-        load_wo(0)
-        load_wo(1)
-        load_wo(2)
-        load_wo(3)
-        for i in range(3, T_TILES):
+        for head in range(HEADS):
+            load_wo(head, 0)
+        load_x(3)
+        load_o(3)
+        for head in range(HEADS):
+            load_wo(head, 1)
+        for i in range(4, T_TILES):
             load_x(i)
             load_o(i)
 
@@ -193,18 +196,12 @@ def tile_multiscaleretention_pc_kernel(tc, o_ret, x, Wg, gn_weight, Wo, out):
 
         wo_grouped = {}
 
-        def regroup_wo_on_scalar(head):
-            wo_grouped[(head, 0)] = regroup(nc.scalar.copy, wo_raw[head][:, :, 0:N_TILE])
-            if head % 2 == 1:
-                wo_grouped[(head, 1)] = regroup(nc.scalar.copy, wo_raw[head][:, :, N_TILE:N_OUT])
+        def regroup_wo(copy, head, half):
+            wo_grouped[(head, half)] = regroup(copy, wo_raw[(head, half)][:])
 
-        def regroup_wo_on_vector(head):
-            wo_grouped[(head, 1)] = regroup(nc.vector.tensor_copy, wo_raw[head][:, :, N_TILE:N_OUT])
-
-        def quantise_wo(head):
-            for half in range(N_HALVES):
-                cols = slice(N_TILE * half, N_TILE * (half + 1))
-                quantise_weights(wo_grouped[(head, half)], wo_codes[:, head, cols], wo_scales[:, head, cols])
+        def quantise_wo(head, half):
+            cols = slice(N_TILE * half, N_TILE * (half + 1))
+            quantise_weights(wo_grouped[(head, half)], wo_codes[:, head, cols], wo_scales[:, head, cols])
 
         h_codes = keep.tile([P, T_TILES, HEADS, P], U32, align_bytes=64)
         h_scales = keep.tile([P, T_TILES, HEADS, P], U8, align_bytes=64)
@@ -217,7 +214,7 @@ def tile_multiscaleretention_pc_kernel(tc, o_ret, x, Wg, gn_weight, Wo, out):
         def weigh_o(i):
             for head in range(HEADS):
                 og = og_pool.tile([P, 2, P, 2], F32, tag="og")
-                engine = nc.gpsimd if head == HEADS - 1 and i > 0 else nc.vector
+                engine = nc.gpsimd if head >= 2 and i > 0 else nc.vector
                 engine.tensor_tensor(
                     out=og[:],
                     in0=in_word_order(o_raw[:, i, DV * head : DV * (head + 1)]),
@@ -278,41 +275,38 @@ def tile_multiscaleretention_pc_kernel(tc, o_ret, x, Wg, gn_weight, Wo, out):
                 in_=h_grouped_tiles[i][:, heads, :, :].rearrange("p h t j -> p (h t j)"),
             )
 
-        def project_head(acc, i, head, half):
+        def project(acc, i, half, heads):
             cols = slice(N_TILE * half, N_TILE * (half + 1))
-            nc.tensor.matmul_mx(
-                out=acc[half][:],
-                lhsT=h_codes[:, i, head, :].bitcast(FP8X4),
-                lhsT_scale=h_scales[:, i, head, :],
-                rhs=wo_codes[:, head, cols].bitcast(FP8X4),
-                rhs_scale=wo_scales[:, head, cols],
-                start=(head == 0),
-                stop=(head == HEADS - 1),
-            )
+            for head in heads:
+                nc.tensor.matmul_mx(
+                    out=acc[:],
+                    lhsT=h_codes[:, i, head, :].bitcast(FP8X4),
+                    lhsT_scale=h_scales[:, i, head, :],
+                    rhs=wo_codes[:, head, cols].bitcast(FP8X4),
+                    rhs_scale=wo_scales[:, head, cols],
+                    start=(head == 0),
+                    stop=(head == HEADS - 1),
+                )
+
+        def store(acc, i, half, copy):
+            result = result_pool.tile([P, N_TILE], F32, name="result", tag="result")
+            copy(out=result[:], in_=acc[:])
+            nc.sync.dma_start(out=out_view[:, i, N_TILE * half : N_TILE * (half + 1)], in_=result[:])
+
+        def project_and_store(i, half):
+            acc = psum_acc.tile([P, N_TILE], F32, name="acc", tag="acc")
+            project(acc, i, half, range(HEADS))
+            store(acc, i, half, nc.scalar.copy)
 
         def finish_last_tile(i):
-            acc = [psum_acc.tile([P, N_TILE], F32, name="acc%d" % half, tag="acc") for half in range(N_HALVES)]
+            acc = [psum_acc.tile([P, N_TILE], F32, name="acc", tag="acc") for half in range(N_HALVES)]
             for first in (0, 2):
                 quantise_h(i, slice(first, first + 2))
             for first in (0, 2):
                 for half in range(N_HALVES):
-                    for head in (first, first + 1):
-                        project_head(acc, i, head, half)
-            for half, copy in enumerate((nc.vector.tensor_copy, nc.scalar.copy)):
-                cols = slice(N_TILE * half, N_TILE * (half + 1))
-                result = pair.tile([P, N_TILE], F32, name="last_result", tag="last_result")
-                copy(out=result[:], in_=acc[half][:])
-                nc.sync.dma_start(out=out_view[:, i, cols], in_=result[:])
-
-        def project_and_store(i):
-            acc = [psum_acc.tile([P, N_TILE], F32, name="acc%d" % half, tag="acc") for half in range(N_HALVES)]
-            for head in range(HEADS):
-                for half in range(N_HALVES):
-                    project_head(acc, i, head, half)
-            result = pair.tile([P, N_OUT], F32, tag="result")
-            for half in range(N_HALVES):
-                nc.scalar.copy(out=result[:, N_TILE * half : N_TILE * (half + 1)], in_=acc[half][:])
-            nc.sync.dma_start(out=out_view[:, i, :], in_=result[:])
+                    project(acc[half], i, half, (first, first + 1))
+            store(acc[0], i, 0, nc.vector.tensor_copy)
+            store(acc[1], i, 1, nc.scalar.copy)
 
         with tc.manual_schedule(engines={mybir.EngineType.PE, mybir.EngineType.DVE, mybir.EngineType.Activation}):
             spread_gn()
@@ -354,32 +348,37 @@ def tile_multiscaleretention_pc_kernel(tc, o_ret, x, Wg, gn_weight, Wo, out):
         for step in range(1, T_TILES + 1):
             if step + 2 < T_TILES:
                 transpose_x(step + 2)
-            if step + 1 < T_TILES:
-                square_o(step + 1)
             transpose_h_words(step - 1)
             copy_h_words(step - 1)
             if step < T_TILES:
                 gate_matmul(step, 0)
                 gate_matmul(step, 1)
-            if step <= 2:
-                regroup_wo_on_scalar(2 * step - 2)
-                regroup_wo_on_scalar(2 * step - 1)
-                regroup_wo_on_vector(2 * step - 2)
-                quantise_wo(2 * step - 2)
-                quantise_wo(2 * step - 1)
+            if step == 1:
+                for head in range(HEADS):
+                    regroup_wo(nc.scalar.copy, head, 0)
+                    quantise_wo(head, 0)
+            if step + 1 < T_TILES:
+                square_o(step + 1)
             if step >= 2:
-                project_and_store(step - 2)
+                project_and_store(step - 2, 0)
             if step < T_TILES:
                 gate_matmul(step, 2)
                 gate_matmul(step, 3)
+            if step in (3, 4):
+                for head in (2 * step - 6, 2 * step - 5):
+                    regroup_wo(nc.vector.tensor_copy, head, 1)
+                    quantise_wo(head, 1)
+            if step == 4:
+                project_and_store(0, 1)
+            if step >= 4:
+                project_and_store(step - 3, 1)
             if step + 2 < T_TILES:
                 quantise_x(step + 2)
             if step < T_TILES:
                 quantise_h(step - 1)
-            else:
-                finish_last_tile(step - 1)
-            if step < T_TILES:
                 for head in range(HEADS):
                     gate_times_weighed_norm(step, head)
-                if step + 1 < T_TILES:
-                    weigh_o(step + 1)
+            if step + 1 < T_TILES:
+                weigh_o(step + 1)
+        project_and_store(T_TILES - 2, 1)
+        finish_last_tile(T_TILES - 1)

@@ -23,7 +23,8 @@ T_TILES = T // P
 E_PASSES = E // K_PASS
 N_HALVES = N_OUT // N_TILE
 EPS = 1e-5
-OG_TILES = 4
+GPSIMD_FROM = 3
+OG_TILES = 3
 
 FLOPS = 2 * T * E * F + 2 * T * F * N_OUT
 
@@ -34,10 +35,10 @@ def tile_multiscaleretention_pc_kernel(tc, o_ret, x, Wg, gn_weight, Wo, out):
     o_view = o_ret.rearrange("b t h d -> (b t) (h d)").rearrange("(p i) f -> p i f", i=T_TILES)
     out_view = out.flatten_outer_dims().rearrange("(p i) n -> p i n", i=T_TILES)
 
-    with tc.tile_pool(name="keep", bufs=1) as keep, tc.tile_pool(name="w_stage", bufs=4) as w_stage, tc.tile_pool(
-        name="w_raw", bufs=5
+    with tc.tile_pool(name="keep", bufs=1) as keep, tc.tile_pool(name="w_stage", bufs=3) as w_stage, tc.tile_pool(
+        name="w_raw", bufs=4
     ) as w_raw, tc.tile_pool(name="x_pool", bufs=4) as x_pool, tc.tile_pool(
-        name="og_pool", bufs=OG_TILES * HEADS
+        name="og_pool", bufs=OG_TILES
     ) as og_pool, tc.tile_pool(name="hb_pool", bufs=2 * HEADS) as hb_pool, tc.tile_pool(name="pair", bufs=2) as pair, tc.tile_pool(name="result_pool", bufs=4) as result_pool, tc.psum_pool(name="psum_g", bufs=3) as psum_g, tc.psum_pool(
         name="psum_ht", bufs=2
     ) as psum_ht, tc.psum_pool(name="psum_xt", bufs=1) as psum_xt, tc.psum_pool(
@@ -160,48 +161,57 @@ def tile_multiscaleretention_pc_kernel(tc, o_ret, x, Wg, gn_weight, Wo, out):
 
         wg_codes = keep.tile([P, E_PASSES, F], U32, align_bytes=64)
         wg_scales = keep.tile([P, E_PASSES, F], U8, align_bytes=64)
-        wo_codes = keep.tile([P, HEADS, N_OUT], U32, align_bytes=64)
-        wo_scales = keep.tile([P, HEADS, N_OUT], U8, align_bytes=64)
+        wo_codes = keep.tile([P, N_HALVES, HEADS, N_TILE], U32, align_bytes=64)
+        wo_scales = keep.tile([P, N_HALVES, HEADS, N_TILE], U8, align_bytes=64)
 
-        def regroup(copy, rows):
-            grouped = w_stage.tile([P, N_TILE, PACK], BF16, align_bytes=64, tag="w_grouped")
+        def new_weights():
+            return w_stage.tile([P, 2, N_TILE, PACK], BF16, align_bytes=64, name="w_grouped", tag="w_grouped")
+
+        def regroup(copy, grouped, rows):
             copy(
-                out=grouped[:].rearrange("p (c i) j -> p c j i", i=4),
+                out=grouped.rearrange("p (c i) j -> p c j i", i=4),
                 in_=rows.rearrange("p j (c i) -> p c j i", i=4),
             )
-            return grouped
 
-        def regroup_in_word_order(copy, rows):
-            grouped = w_stage.tile([P, N_TILE, PACK], BF16, align_bytes=64, tag="w_grouped")
+        def regroup_in_word_order(copy, grouped, rows):
             copy(
-                out=grouped[:].rearrange("p (u c e) j -> p c j u e", u=2, e=2),
+                out=grouped.rearrange("p (u c e) j -> p c j u e", u=2, e=2),
                 in_=rows.rearrange("p j (c u e) -> p c j u e", u=2, e=2),
             )
-            return grouped
 
         def quantise_weights(grouped, codes, scales):
             nc.vector.quantize_mx(
-                out=codes.bitcast(FP8X4), scales=scales, in_=grouped[:].rearrange("p w j -> p (w j)")
+                out=codes.bitcast(FP8X4), scales=scales, in_=grouped[:].rearrange("p h w j -> p (h w j)")
             )
 
         wg_grouped = {}
 
         def regroup_wg(copy, c, head):
-            first = DV * (head % 2)
-            wg_grouped[(c, head)] = regroup_in_word_order(copy, wg_raw[(c, head // 2)][:, :, first : first + DV])
+            pair_of_heads, odd = divmod(head, 2)
+            if (c, pair_of_heads) not in wg_grouped:
+                wg_grouped[(c, pair_of_heads)] = new_weights()
+            rows = wg_raw[(c, pair_of_heads)][:, :, DV * odd : DV * (odd + 1)]
+            regroup_in_word_order(copy, wg_grouped[(c, pair_of_heads)][:, odd, :, :], rows)
 
-        def quantise_wg(c, head):
-            cols = slice(DV * head, DV * (head + 1))
-            quantise_weights(wg_grouped[(c, head)], wg_codes[:, c, cols], wg_scales[:, c, cols])
+        def quantise_wg(c, pair_of_heads):
+            cols = slice(2 * DV * pair_of_heads, 2 * DV * (pair_of_heads + 1))
+            quantise_weights(wg_grouped[(c, pair_of_heads)], wg_codes[:, c, cols], wg_scales[:, c, cols])
 
         wo_grouped = {}
 
         def regroup_wo(copy, head, half):
-            wo_grouped[(head, half)] = regroup(copy, wo_raw[(head, half)][:])
+            pair_of_heads, odd = divmod(head, 2)
+            if (pair_of_heads, half) not in wo_grouped:
+                wo_grouped[(pair_of_heads, half)] = new_weights()
+            regroup(copy, wo_grouped[(pair_of_heads, half)][:, odd, :, :], wo_raw[(head, half)][:])
 
-        def quantise_wo(head, half):
-            cols = slice(N_TILE * half, N_TILE * (half + 1))
-            quantise_weights(wo_grouped[(head, half)], wo_codes[:, head, cols], wo_scales[:, head, cols])
+        def quantise_wo(pair_of_heads, half):
+            heads = slice(2 * pair_of_heads, 2 * pair_of_heads + 2)
+            quantise_weights(
+                wo_grouped[(pair_of_heads, half)],
+                wo_codes[:, half, heads, :].rearrange("p h n -> p (h n)"),
+                wo_scales[:, half, heads, :].rearrange("p h n -> p (h n)"),
+            )
 
         h_codes = keep.tile([P, T_TILES, HEADS, P], U32, align_bytes=64)
         h_scales = keep.tile([P, T_TILES, HEADS, P], U8, align_bytes=64)
@@ -212,17 +222,18 @@ def tile_multiscaleretention_pc_kernel(tc, o_ret, x, Wg, gn_weight, Wo, out):
         ht_banks = {}
 
         def weigh_o(i):
-            for head in range(HEADS):
-                og = og_pool.tile([P, 2, P, 2], F32, tag="og")
-                engine = nc.gpsimd if head >= 2 and i > 0 else nc.vector
-                engine.tensor_tensor(
-                    out=og[:],
-                    in0=in_word_order(o_raw[:, i, DV * head : DV * (head + 1)]),
-                    in1=gn_all[:],
-                    op=ALU.mult,
-                )
-                og_tiles[(i, head)] = og
-
+            og = og_pool.tile([P, 2, HEADS, P, 2], F32, tag="og")
+            o_words = o_raw[:, i, :].rearrange("t (h p u e) -> t u h p e", h=HEADS, u=2, e=2)
+            shares = [(nc.vector, 0, 4)] if i < GPSIMD_FROM else [(nc.vector, 0, 2), (nc.gpsimd, 2, 4)]
+            for engine, first, end in shares:
+                for u in range(2):
+                    engine.tensor_tensor(
+                        out=og[:, u, first:end, :, :],
+                        in0=o_words[:, u, first:end, :, :],
+                        in1=gn_all[:, u, :, :].unsqueeze(1).to_broadcast([P, end - first, P, 2]),
+                        op=ALU.mult,
+                    )
+            og_tiles[i] = og
 
         def gate_matmul(i, head):
             cols = slice(DV * head, DV * (head + 1))
@@ -242,10 +253,10 @@ def tile_multiscaleretention_pc_kernel(tc, o_ret, x, Wg, gn_weight, Wo, out):
         def gate_times_weighed_norm(i, head):
             h0 = hb_pool.tile([P, DV], BF16, tag="hb")
             nc.vector.scalar_tensor_tensor(
-                out=h0[:],
-                in0=g_banks[(i, head)][:],
+                out=h0[:].rearrange("t (u w) -> t u w", u=2),
+                in0=g_banks[(i, head)][:].rearrange("t (u w) -> t u w", u=2),
                 scalar=rinv[i][:, head : head + 1],
-                in1=og_tiles[(i, head)][:].rearrange("t u p e -> t (u p e)"),
+                in1=og_tiles[i][:, :, head, :, :].rearrange("t u p e -> t u (p e)"),
                 op0=ALU.mult,
                 op1=ALU.mult,
             )
@@ -276,14 +287,13 @@ def tile_multiscaleretention_pc_kernel(tc, o_ret, x, Wg, gn_weight, Wo, out):
             )
 
         def project(acc, i, half, heads):
-            cols = slice(N_TILE * half, N_TILE * (half + 1))
             for head in heads:
                 nc.tensor.matmul_mx(
                     out=acc[:],
                     lhsT=h_codes[:, i, head, :].bitcast(FP8X4),
                     lhsT_scale=h_scales[:, i, head, :],
-                    rhs=wo_codes[:, head, cols].bitcast(FP8X4),
-                    rhs_scale=wo_scales[:, head, cols],
+                    rhs=wo_codes[:, half, head, :].bitcast(FP8X4),
+                    rhs_scale=wo_scales[:, half, head, :],
                     start=(head == 0),
                     stop=(head == HEADS - 1),
                 )
@@ -318,11 +328,9 @@ def tile_multiscaleretention_pc_kernel(tc, o_ret, x, Wg, gn_weight, Wo, out):
                 regroup_wg(nc.scalar.copy, c, 1)
             transpose_x(1)
             regroup_wg(nc.vector.tensor_copy, 0, 0)
-            quantise_wg(0, 0)
             regroup_wg(nc.vector.tensor_copy, 1, 0)
-            quantise_wg(0, 1)
+            quantise_wg(0, 0)
             quantise_wg(1, 0)
-            quantise_wg(1, 1)
             gate_matmul(0, 0)
             gate_matmul(0, 1)
             gate_times_weighed_norm(0, 0)
@@ -334,11 +342,9 @@ def tile_multiscaleretention_pc_kernel(tc, o_ret, x, Wg, gn_weight, Wo, out):
             regroup_wg(nc.scalar.copy, 1, 3)
             weigh_o(1)
             regroup_wg(nc.vector.tensor_copy, 0, 2)
-            quantise_wg(0, 2)
             regroup_wg(nc.vector.tensor_copy, 1, 2)
-            quantise_wg(0, 3)
-            quantise_wg(1, 2)
-            quantise_wg(1, 3)
+            quantise_wg(0, 1)
+            quantise_wg(1, 1)
             quantise_x(2)
             gate_matmul(0, 2)
             gate_matmul(0, 3)
@@ -354,9 +360,10 @@ def tile_multiscaleretention_pc_kernel(tc, o_ret, x, Wg, gn_weight, Wo, out):
                 gate_matmul(step, 0)
                 gate_matmul(step, 1)
             if step == 1:
-                for head in range(HEADS):
-                    regroup_wo(nc.scalar.copy, head, 0)
-                    quantise_wo(head, 0)
+                for pair_of_heads in range(2):
+                    regroup_wo(nc.scalar.copy, 2 * pair_of_heads, 0)
+                    regroup_wo(nc.scalar.copy, 2 * pair_of_heads + 1, 0)
+                    quantise_wo(pair_of_heads, 0)
             if step + 1 < T_TILES:
                 square_o(step + 1)
             if step >= 2:
@@ -365,9 +372,10 @@ def tile_multiscaleretention_pc_kernel(tc, o_ret, x, Wg, gn_weight, Wo, out):
                 gate_matmul(step, 2)
                 gate_matmul(step, 3)
             if step in (3, 4):
-                for head in (2 * step - 6, 2 * step - 5):
-                    regroup_wo(nc.vector.tensor_copy, head, 1)
-                    quantise_wo(head, 1)
+                pair_of_heads = step - 3
+                regroup_wo(nc.scalar.copy, 2 * pair_of_heads, 1)
+                regroup_wo(nc.vector.tensor_copy, 2 * pair_of_heads + 1, 1)
+                quantise_wo(pair_of_heads, 1)
             if step == 4:
                 project_and_store(0, 1)
             if step >= 4:

@@ -224,7 +224,7 @@ def tile_multiscaleretention_pc_kernel(tc, o_ret, x, Wg, gn_weight, Wo, out):
         def weigh_o(i):
             og = og_pool.tile([P, 2, HEADS, P, 2], F32, tag="og")
             o_words = o_raw[:, i, :].rearrange("t (h p u e) -> t u h p e", h=HEADS, u=2, e=2)
-            shares = [(nc.vector, 0, 4)] if i < GPSIMD_FROM else [(nc.vector, 0, 2), (nc.gpsimd, 2, 4)]
+            shares = [(nc.vector, 0, 4)] if i < GPSIMD_FROM else [(nc.vector, 0, 2), (nc.gpsimd, 2, 3), (nc.gpsimd, 3, 4)]
             for engine, first, end in shares:
                 for u in range(2):
                     engine.tensor_tensor(

@@ -24,6 +24,7 @@ E_PASSES = E // K_PASS
 N_HALVES = N_OUT // N_TILE
 EPS = 1e-5
 GPSIMD_FROM = 3
+SECOND_HALF = 3
 OG_TILES = 3
 
 FLOPS = 2 * T * E * F + 2 * T * F * N_OUT
@@ -40,8 +41,8 @@ def tile_multiscaleretention_pc_kernel(tc, o_ret, x, Wg, gn_weight, Wo, out):
     ) as w_raw, tc.tile_pool(name="x_pool", bufs=4) as x_pool, tc.tile_pool(
         name="og_pool", bufs=OG_TILES
     ) as og_pool, tc.tile_pool(name="hb_pool", bufs=2 * HEADS) as hb_pool, tc.tile_pool(name="pair", bufs=2) as pair, tc.tile_pool(name="result_pool", bufs=4) as result_pool, tc.psum_pool(name="psum_g", bufs=3) as psum_g, tc.psum_pool(
-        name="psum_ht", bufs=2
-    ) as psum_ht, tc.psum_pool(name="psum_xt", bufs=1) as psum_xt, tc.psum_pool(
+        name="psum_t", bufs=3
+    ) as psum_t, tc.psum_pool(
         name="psum_acc", bufs=2
     ) as psum_acc:
         gn_cols = keep.tile([P, PACK], BF16)
@@ -108,7 +109,7 @@ def tile_multiscaleretention_pc_kernel(tc, o_ret, x, Wg, gn_weight, Wo, out):
         gn_all = keep.tile([P, 2, P, 2], F32)
 
         def spread_gn():
-            gn_bank = psum_xt.tile([P, PACK, P], F32, tag="xt")
+            gn_bank = psum_t.tile([P, PACK, P], F32, tag="t")
             for j in range(PACK):
                 nc.tensor.matmul(
                     out=gn_bank[:, j, :],
@@ -125,7 +126,7 @@ def tile_multiscaleretention_pc_kernel(tc, o_ret, x, Wg, gn_weight, Wo, out):
         rinv = {}
 
         def transpose_x(i):
-            xt = psum_xt.tile([P, PACK, P], F32, tag="xt")
+            xt = psum_t.tile([P, PACK, P], F32, tag="t")
             x_words = x_raw[i][:].bitcast(F32)
             for c in range(E_PASSES):
                 for u in range(2):
@@ -265,7 +266,7 @@ def tile_multiscaleretention_pc_kernel(tc, o_ret, x, Wg, gn_weight, Wo, out):
         def transpose_h_words(i):
             h_grouped_tiles[i] = pair.tile([P, HEADS, P, PACK], BF16, align_bytes=64, tag="h_grouped", name="h_grouped")
             for pair_of_heads in range(2):
-                ht = psum_ht.tile([P, PACK, P], F32, tag="ht")
+                ht = psum_t.tile([P, PACK, P], F32, tag="t")
                 for hu in range(PACK):
                     words = h0_tiles[(i, 2 * pair_of_heads + hu // 2)][:].bitcast(F32)
                     u = hu % 2
@@ -303,7 +304,10 @@ def tile_multiscaleretention_pc_kernel(tc, o_ret, x, Wg, gn_weight, Wo, out):
             copy(out=result[:], in_=acc[:])
             nc.sync.dma_start(out=out_view[:, i, N_TILE * half : N_TILE * (half + 1)], in_=result[:])
 
+        tiles_done = [0, 0]
+
         def project_and_store(i, half):
+            tiles_done[half] += 1
             acc = psum_acc.tile([P, N_TILE], F32, name="acc", tag="acc")
             project(acc, i, half, range(HEADS))
             store(acc, i, half, nc.scalar.copy)
@@ -337,10 +341,9 @@ def tile_multiscaleretention_pc_kernel(tc, o_ret, x, Wg, gn_weight, Wo, out):
             quantise_x(1)
             gate_times_weighed_norm(0, 1)
             regroup_wg(nc.scalar.copy, 0, 3)
-            square_o(1)
             transpose_x(2)
             regroup_wg(nc.scalar.copy, 1, 3)
-            weigh_o(1)
+            square_o(1)
             regroup_wg(nc.vector.tensor_copy, 0, 2)
             regroup_wg(nc.vector.tensor_copy, 1, 2)
             quantise_wg(0, 1)
@@ -350,12 +353,13 @@ def tile_multiscaleretention_pc_kernel(tc, o_ret, x, Wg, gn_weight, Wo, out):
             gate_matmul(0, 3)
             gate_times_weighed_norm(0, 2)
             gate_times_weighed_norm(0, 3)
+            weigh_o(1)
 
         for step in range(1, T_TILES + 1):
-            if step + 2 < T_TILES:
-                transpose_x(step + 2)
             transpose_h_words(step - 1)
             copy_h_words(step - 1)
+            if step + 2 < T_TILES:
+                transpose_x(step + 2)
             if step < T_TILES:
                 gate_matmul(step, 0)
                 gate_matmul(step, 1)
@@ -371,15 +375,9 @@ def tile_multiscaleretention_pc_kernel(tc, o_ret, x, Wg, gn_weight, Wo, out):
             if step < T_TILES:
                 gate_matmul(step, 2)
                 gate_matmul(step, 3)
-            if step in (3, 4):
-                pair_of_heads = step - 3
-                regroup_wo(nc.scalar.copy, 2 * pair_of_heads, 1)
-                regroup_wo(nc.vector.tensor_copy, 2 * pair_of_heads + 1, 1)
-                quantise_wo(pair_of_heads, 1)
-            if step == 4:
-                project_and_store(0, 1)
-            if step >= 4:
-                project_and_store(step - 3, 1)
+            if step > SECOND_HALF + 1:
+                while tiles_done[1] <= step - 3:
+                    project_and_store(tiles_done[1], 1)
             if step + 2 < T_TILES:
                 quantise_x(step + 2)
             if step < T_TILES:
@@ -388,5 +386,11 @@ def tile_multiscaleretention_pc_kernel(tc, o_ret, x, Wg, gn_weight, Wo, out):
                     gate_times_weighed_norm(step, head)
             if step + 1 < T_TILES:
                 weigh_o(step + 1)
+            if step in (SECOND_HALF, SECOND_HALF + 1):
+                pair_of_heads = step - SECOND_HALF
+                regroup_wo(nc.vector.tensor_copy, 2 * pair_of_heads, 1)
+                copy = nc.vector.tensor_copy if pair_of_heads == 0 else nc.scalar.copy
+                regroup_wo(copy, 2 * pair_of_heads + 1, 1)
+                quantise_wo(pair_of_heads, 1)
         project_and_store(T_TILES - 2, 1)
         finish_last_tile(T_TILES - 1)

@@ -120,8 +120,8 @@ def tile_multiscaleretention_pc_kernel(tc, o_ret, x, Wg, gn_weight, Wo, out):
                 )
             nc.vector.tensor_copy(out=gn_all[:], in_=gn_bank[:].rearrange("t (u e) p -> t u p e", e=2))
 
-        x_codes = keep.tile([P, T_TILES, E_PASSES, P], U32, align_bytes=64)
-        x_scales = keep.tile([P, T_TILES, E_PASSES, P], U8, align_bytes=64)
+        x_codes = keep.tile([P, T_TILES, E_PASSES, P], U32, align_bytes=256)
+        x_scales = keep.tile([P, T_TILES, E_PASSES, P], U8, align_bytes=256)
         x_grouped = {}
         rinv = {}
 
@@ -160,10 +160,10 @@ def tile_multiscaleretention_pc_kernel(tc, o_ret, x, Wg, gn_weight, Wo, out):
                 in_=x_grouped[i][:].rearrange("p c t j -> p (c t j)"),
             )
 
-        wg_codes = keep.tile([P, E_PASSES, F], U32, align_bytes=64)
-        wg_scales = keep.tile([P, E_PASSES, F], U8, align_bytes=64)
-        wo_codes = keep.tile([P, N_HALVES, HEADS, N_TILE], U32, align_bytes=64)
-        wo_scales = keep.tile([P, N_HALVES, HEADS, N_TILE], U8, align_bytes=64)
+        wg_codes = keep.tile([P, E_PASSES, F], U32, align_bytes=256)
+        wg_scales = keep.tile([P, E_PASSES, F], U8, align_bytes=256)
+        wo_codes = keep.tile([P, N_HALVES, HEADS, N_TILE], U32, align_bytes=256)
+        wo_scales = keep.tile([P, N_HALVES, HEADS, N_TILE], U8, align_bytes=256)
 
         def new_weights():
             return w_stage.tile([P, 2, N_TILE, PACK], BF16, align_bytes=64, name="w_grouped", tag="w_grouped")
@@ -214,8 +214,8 @@ def tile_multiscaleretention_pc_kernel(tc, o_ret, x, Wg, gn_weight, Wo, out):
                 wo_scales[:, half, heads, :].rearrange("p h n -> p (h n)"),
             )
 
-        h_codes = keep.tile([P, T_TILES, HEADS, P], U32, align_bytes=64)
-        h_scales = keep.tile([P, T_TILES, HEADS, P], U8, align_bytes=64)
+        h_codes = keep.tile([P, T_TILES, HEADS, P], U32, align_bytes=256)
+        h_scales = keep.tile([P, T_TILES, HEADS, P], U8, align_bytes=256)
         g_banks = {}
         h0_tiles = {}
         og_tiles = {}

@@ -25,7 +25,7 @@ N_HALVES = N_OUT // N_TILE
 EPS = 1e-5
 GPSIMD_FROM = 3
 SECOND_HALF = 3
-OG_TILES = 3
+OG_TILES = 2
 
 FLOPS = 2 * T * E * F + 2 * T * F * N_OUT
 
@@ -40,7 +40,7 @@ def tile_multiscaleretention_pc_kernel(tc, o_ret, x, Wg, gn_weight, Wo, out):
         name="w_raw", bufs=4
     ) as w_raw, tc.tile_pool(name="x_pool", bufs=4) as x_pool, tc.tile_pool(
         name="og_pool", bufs=OG_TILES
-    ) as og_pool, tc.tile_pool(name="hb_pool", bufs=2 * HEADS) as hb_pool, tc.tile_pool(name="pair", bufs=2) as pair, tc.tile_pool(name="result_pool", bufs=4) as result_pool, tc.psum_pool(name="psum_g", bufs=3) as psum_g, tc.psum_pool(
+    ) as og_pool, tc.tile_pool(name="hb_pool", bufs=2 * HEADS) as hb_pool, tc.tile_pool(name="pair", bufs=2) as pair, tc.tile_pool(name="result_pool", bufs=6) as result_pool, tc.psum_pool(name="psum_g", bufs=3) as psum_g, tc.psum_pool(
         name="psum_t", bufs=3
     ) as psum_t, tc.psum_pool(
         name="psum_acc", bufs=2

@@ -23,7 +23,6 @@ T_TILES = T // P
 E_PASSES = E // K_PASS
 N_HALVES = N_OUT // N_TILE
 EPS = 1e-5
-GPSIMD_FROM = 3
 SECOND_HALF = 3
 OG_TILES = 2
 
@@ -225,15 +224,13 @@ def tile_multiscaleretention_pc_kernel(tc, o_ret, x, Wg, gn_weight, Wo, out):
         def weigh_o(i):
             og = og_pool.tile([P, 2, HEADS, P, 2], F32, tag="og")
             o_words = o_raw[:, i, :].rearrange("t (h p u e) -> t u h p e", h=HEADS, u=2, e=2)
-            shares = [(nc.vector, 0, 4)] if i < GPSIMD_FROM else [(nc.vector, 0, 2), (nc.gpsimd, 2, 3), (nc.gpsimd, 3, 4)]
-            for engine, first, end in shares:
-                for u in range(2):
-                    engine.tensor_tensor(
-                        out=og[:, u, first:end, :, :],
-                        in0=o_words[:, u, first:end, :, :],
-                        in1=gn_all[:, u, :, :].unsqueeze(1).to_broadcast([P, end - first, P, 2]),
-                        op=ALU.mult,
-                    )
+            for u in range(2):
+                nc.vector.tensor_tensor(
+                    out=og[:, u, :, :, :],
+                    in0=o_words[:, u, :, :, :],
+                    in1=gn_all[:, u, :, :].unsqueeze(1).to_broadcast([P, HEADS, P, 2]),
+                    op=ALU.mult,
+                )
             og_tiles[i] = og
 
         def gate_matmul(i, head):
@@ -388,9 +385,8 @@ def tile_multiscaleretention_pc_kernel(tc, o_ret, x, Wg, gn_weight, Wo, out):
                 weigh_o(step + 1)
             if step in (SECOND_HALF, SECOND_HALF + 1):
                 pair_of_heads = step - SECOND_HALF
-                regroup_wo(nc.vector.tensor_copy, 2 * pair_of_heads, 1)
-                copy = nc.vector.tensor_copy if pair_of_heads == 0 else nc.scalar.copy
-                regroup_wo(copy, 2 * pair_of_heads + 1, 1)
+                regroup_wo(nc.scalar.copy, 2 * pair_of_heads, 1)
+                regroup_wo(nc.vector.tensor_copy, 2 * pair_of_heads + 1, 1)
                 quantise_wo(pair_of_heads, 1)
         project_and_store(T_TILES - 2, 1)
         finish_last_tile(T_TILES - 1)

@@ -23,7 +23,6 @@ T_TILES = T // P
 E_PASSES = E // K_PASS
 N_HALVES = N_OUT // N_TILE
 EPS = 1e-5
-SECOND_HALF = 3
 OG_TILES = 2
 
 FLOPS = 2 * T * E * F + 2 * T * F * N_OUT
@@ -36,14 +35,12 @@ def tile_multiscaleretention_pc_kernel(tc, o_ret, x, Wg, gn_weight, Wo, out):
     out_view = out.flatten_outer_dims().rearrange("(p i) n -> p i n", i=T_TILES)
 
     with tc.tile_pool(name="keep", bufs=1) as keep, tc.tile_pool(name="w_stage", bufs=3) as w_stage, tc.tile_pool(
-        name="w_raw", bufs=4
+        name="w_raw", bufs=6
     ) as w_raw, tc.tile_pool(name="x_pool", bufs=4) as x_pool, tc.tile_pool(
         name="og_pool", bufs=OG_TILES
     ) as og_pool, tc.tile_pool(name="hb_pool", bufs=2 * HEADS) as hb_pool, tc.tile_pool(name="pair", bufs=2) as pair, tc.tile_pool(name="result_pool", bufs=6) as result_pool, tc.psum_pool(name="psum_g", bufs=3) as psum_g, tc.psum_pool(
-        name="psum_t", bufs=3
-    ) as psum_t, tc.psum_pool(
-        name="psum_acc", bufs=2
-    ) as psum_acc:
+        name="psum_t", bufs=5
+    ) as psum_t:
         gn_cols = keep.tile([P, PACK], BF16)
         ident = keep.tile([P, P], F32)
         make_identity(nc, ident[:])
@@ -63,15 +60,16 @@ def tile_multiscaleretention_pc_kernel(tc, o_ret, x, Wg, gn_weight, Wo, out):
             x_raw[i] = x_pool.tile([P, E], BF16, name="x_raw", tag="x_raw")
             nc.sync.dma_start(out=x_raw[i][:], in_=x_view[:, i, :])
 
-        def load_o(i):
-            nc.sync.dma_start(out=o_raw[:, i, :], in_=o_view[:, i, :])
+        def load_o(i, heads=slice(0, HEADS)):
+            cols = slice(DV * heads.start, DV * heads.stop)
+            nc.sync.dma_start(out=o_raw[:, i, cols], in_=o_view[:, i, cols])
 
-        def load_wg(head_pair):
-            cols = slice(2 * DV * head_pair, 2 * DV * (head_pair + 1))
-            for c in range(E_PASSES):
-                wg_raw[(c, head_pair)] = w_raw.tile([P, PACK, 2 * DV], BF16, name="wg_raw", tag="w_raw")
+        def load_wg(c, head_pair, parts=(slice(0, 2 * DV),)):
+            wg_raw[(c, head_pair)] = w_raw.tile([P, PACK, 2 * DV], BF16, name="wg_raw", tag="w_raw")
+            for part in parts:
+                cols = slice(2 * DV * head_pair + part.start, 2 * DV * head_pair + part.stop)
                 nc.sync.dma_start(
-                    out=wg_raw[(c, head_pair)][:],
+                    out=wg_raw[(c, head_pair)][:, :, part],
                     in_=Wg[K_PASS * c : K_PASS * (c + 1), cols].rearrange("(p j) f -> p j f", j=PACK),
                 )
 
@@ -83,22 +81,26 @@ def tile_multiscaleretention_pc_kernel(tc, o_ret, x, Wg, gn_weight, Wo, out):
                 in_=Wo[K_PASS * head : K_PASS * (head + 1), cols].rearrange("(p j) n -> p j n", j=PACK),
             )
 
-        load_x(0)
         nc.sync.dma_start(out=gn_cols[:], in_=gn_weight.rearrange("(p j) -> p j", j=PACK))
-        load_o(0)
-        load_wg(0)
+        load_o(0, slice(0, 2))
+        load_o(0, slice(2, HEADS))
+        load_x(0)
+        load_wg(0, 0, (slice(DV, 2 * DV), slice(0, DV)))
+        load_wg(1, 0)
         load_x(1)
         load_o(1)
         load_x(2)
-        load_wg(1)
+        load_wg(0, 1)
+        load_wg(1, 1)
         load_o(2)
         for head in range(HEADS):
             load_wo(head, 0)
-        load_x(3)
-        load_o(3)
+        for i in range(3, 6):
+            load_x(i)
+            load_o(i)
         for head in range(HEADS):
             load_wo(head, 1)
-        for i in range(4, T_TILES):
+        for i in range(6, T_TILES):
             load_x(i)
             load_o(i)
 
@@ -122,6 +124,8 @@ def tile_multiscaleretention_pc_kernel(tc, o_ret, x, Wg, gn_weight, Wo, out):
         x_codes = keep.tile([P, T_TILES, E_PASSES, P], U32, align_bytes=256)
         x_scales = keep.tile([P, T_TILES, E_PASSES, P], U8, align_bytes=256)
         x_grouped = {}
+        xt_banks = {}
+        ssq = {}
         rinv = {}
 
         def transpose_x(i):
@@ -132,24 +136,29 @@ def tile_multiscaleretention_pc_kernel(tc, o_ret, x, Wg, gn_weight, Wo, out):
                     nc.tensor.transpose(
                         xt[:, 2 * c + u, :], x_words[:, 2 * P * c + u : 2 * P * (c + 1) : 2], ident[:]
                     )
-            grouped = pair.tile([P, E_PASSES, P, PACK], BF16, align_bytes=64, tag="x_grouped")
-            copy = nc.vector.tensor_copy if i == 0 else nc.scalar.copy
-            copy(out=grouped[:].bitcast(F32), in_=xt[:].rearrange("p (c u) t -> p c t u", u=2))
+            xt_banks[i] = xt
+
+        def copy_x(copy, i):
+            grouped = pair.tile([P, E_PASSES, P, PACK], BF16, align_bytes=64, tag="x_grouped", name="x_grouped")
+            copy(out=grouped[:].bitcast(F32), in_=xt_banks[i][:].rearrange("p (c u) t -> p c t u", u=2))
             x_grouped[i] = grouped
 
-        def square_o(i):
-            ssq = keep.tile([P, HEADS], F32, name="ssq%d" % i)
-            for head in range(HEADS):
+        def square_o(i, heads=range(HEADS)):
+            if i not in ssq:
+                ssq[i] = keep.tile([P, HEADS], F32, name="ssq%d" % i)
+            for head in heads:
                 squares = pair.tile([P, DV], BF16, tag="squares")
                 nc.scalar.activation(
                     out=squares[:],
                     in_=o_raw[:, i, DV * head : DV * (head + 1)],
                     func=ACT.Square,
-                    accum_out=ssq[:, head : head + 1],
+                    accum_out=ssq[i][:, head : head + 1],
                 )
+
+        def invert_rms(i):
             rinv[i] = keep.tile([P, HEADS], F32, name="rinv%d" % i)
             nc.scalar.activation(
-                out=rinv[i][:], in_=ssq[:], func=ACT.Abs_reciprocal_sqrt, scale=1.0 / DV, bias=eps_col[:]
+                out=rinv[i][:], in_=ssq[i][:], func=ACT.Abs_reciprocal_sqrt, scale=1.0 / DV, bias=eps_col[:]
             )
 
         def quantise_x(i):
@@ -221,17 +230,16 @@ def tile_multiscaleretention_pc_kernel(tc, o_ret, x, Wg, gn_weight, Wo, out):
         h_grouped_tiles = {}
         ht_banks = {}
 
-        def weigh_o(i):
-            og = og_pool.tile([P, 2, HEADS, P, 2], F32, tag="og")
+        def weigh_o(i, heads=slice(0, HEADS)):
+            if i not in og_tiles:
+                og_tiles[i] = og_pool.tile([P, 2, HEADS, P, 2], F32, name="og", tag="og")
             o_words = o_raw[:, i, :].rearrange("t (h p u e) -> t u h p e", h=HEADS, u=2, e=2)
-            for u in range(2):
-                nc.vector.tensor_tensor(
-                    out=og[:, u, :, :, :],
-                    in0=o_words[:, u, :, :, :],
-                    in1=gn_all[:, u, :, :].unsqueeze(1).to_broadcast([P, HEADS, P, 2]),
-                    op=ALU.mult,
-                )
-            og_tiles[i] = og
+            nc.vector.tensor_tensor(
+                out=og_tiles[i][:, :, heads, :, :],
+                in0=o_words[:, :, heads, :, :],
+                in1=gn_all[:].unsqueeze(2).to_broadcast([P, 2, heads.stop - heads.start, P, 2]),
+                op=ALU.mult,
+            )
 
         def gate_matmul(i, head):
             cols = slice(DV * head, DV * (head + 1))
@@ -260,22 +268,23 @@ def tile_multiscaleretention_pc_kernel(tc, o_ret, x, Wg, gn_weight, Wo, out):
             )
             h0_tiles[(i, head)] = h0
 
-        def transpose_h_words(i):
-            h_grouped_tiles[i] = pair.tile([P, HEADS, P, PACK], BF16, align_bytes=64, tag="h_grouped", name="h_grouped")
-            for pair_of_heads in range(2):
-                ht = psum_t.tile([P, PACK, P], F32, tag="t")
-                for hu in range(PACK):
-                    words = h0_tiles[(i, 2 * pair_of_heads + hu // 2)][:].bitcast(F32)
-                    u = hu % 2
-                    nc.tensor.transpose(ht[:, hu, :], words[:, P * u : P * (u + 1)], ident[:])
-                ht_banks[(i, pair_of_heads)] = ht
+        def transpose_h(i, pair_of_heads):
+            ht = psum_t.tile([P, PACK, P], F32, tag="t", name="ht")
+            for hu in range(PACK):
+                words = h0_tiles[(i, 2 * pair_of_heads + hu // 2)][:].bitcast(F32)
+                u = hu % 2
+                nc.tensor.transpose(ht[:, hu, :], words[:, P * u : P * (u + 1)], ident[:])
+            ht_banks[(i, pair_of_heads)] = ht
 
-        def copy_h_words(i):
-            for pair_of_heads in range(2):
-                nc.scalar.copy(
-                    out=h_grouped_tiles[i][:, 2 * pair_of_heads : 2 * pair_of_heads + 2, :, :].bitcast(F32),
-                    in_=ht_banks[(i, pair_of_heads)][:].rearrange("p (h u) t -> p h t u", u=2),
+        def copy_h(i, pair_of_heads):
+            if i not in h_grouped_tiles:
+                h_grouped_tiles[i] = pair.tile(
+                    [P, HEADS, P, PACK], BF16, align_bytes=64, tag="h_grouped", name="h_grouped"
                 )
+            nc.scalar.copy(
+                out=h_grouped_tiles[i][:, 2 * pair_of_heads : 2 * pair_of_heads + 2, :, :].bitcast(F32),
+                in_=ht_banks[(i, pair_of_heads)][:].rearrange("p (h u) t -> p h t u", u=2),
+            )
 
         def quantise_h(i, heads=slice(0, HEADS)):
             nc.vector.quantize_mx(
@@ -284,109 +293,131 @@ def tile_multiscaleretention_pc_kernel(tc, o_ret, x, Wg, gn_weight, Wo, out):
                 in_=h_grouped_tiles[i][:, heads, :, :].rearrange("p h t j -> p (h t j)"),
             )
 
-        def project(acc, i, half, heads):
-            for head in heads:
-                nc.tensor.matmul_mx(
-                    out=acc[:],
-                    lhsT=h_codes[:, i, head, :].bitcast(FP8X4),
-                    lhsT_scale=h_scales[:, i, head, :],
-                    rhs=wo_codes[:, half, head, :].bitcast(FP8X4),
-                    rhs_scale=wo_scales[:, half, head, :],
-                    start=(head == 0),
-                    stop=(head == HEADS - 1),
-                )
+        acc_banks = {}
 
-        def store(acc, i, half, copy):
+        def project(i, half, pairs=(0, 1)):
+            if (i, half) not in acc_banks:
+                acc_banks[(i, half)] = psum_t.tile([P, N_TILE], F32, name="acc", tag="t")
+            for pair_of_heads in pairs:
+                for head in (2 * pair_of_heads, 2 * pair_of_heads + 1):
+                    nc.tensor.matmul_mx(
+                        out=acc_banks[(i, half)][:],
+                        lhsT=h_codes[:, i, head, :].bitcast(FP8X4),
+                        lhsT_scale=h_scales[:, i, head, :],
+                        rhs=wo_codes[:, half, head, :].bitcast(FP8X4),
+                        rhs_scale=wo_scales[:, half, head, :],
+                        start=(head == 0),
+                        stop=(head == HEADS - 1),
+                    )
+
+        def store(copy, i, half):
             result = result_pool.tile([P, N_TILE], F32, name="result", tag="result")
-            copy(out=result[:], in_=acc[:])
+            copy(out=result[:], in_=acc_banks[(i, half)][:])
             nc.sync.dma_start(out=out_view[:, i, N_TILE * half : N_TILE * (half + 1)], in_=result[:])
 
-        tiles_done = [0, 0]
-
-        def project_and_store(i, half):
-            tiles_done[half] += 1
-            acc = psum_acc.tile([P, N_TILE], F32, name="acc", tag="acc")
-            project(acc, i, half, range(HEADS))
-            store(acc, i, half, nc.scalar.copy)
-
-        def finish_last_tile(i):
-            acc = [psum_acc.tile([P, N_TILE], F32, name="acc", tag="acc") for half in range(N_HALVES)]
-            for first in (0, 2):
-                quantise_h(i, slice(first, first + 2))
-            for first in (0, 2):
-                for half in range(N_HALVES):
-                    project(acc[half], i, half, (first, first + 1))
-            store(acc[0], i, 0, nc.vector.tensor_copy)
-            store(acc[1], i, 1, nc.scalar.copy)
-
+        vector, scalar = nc.vector.tensor_copy, nc.scalar.copy
+        stt = gate_times_weighed_norm
         with tc.manual_schedule(engines={mybir.EngineType.PE, mybir.EngineType.DVE, mybir.EngineType.Activation}):
             spread_gn()
             transpose_x(0)
             square_o(0)
+            invert_rms(0)
+            weigh_o(0, slice(0, 2))
+            weigh_o(0, slice(2, HEADS))
+            copy_x(vector, 0)
             quantise_x(0)
-            weigh_o(0)
-            for c in range(E_PASSES):
-                regroup_wg(nc.scalar.copy, c, 1)
+            regroup_wg(scalar, 0, 1)
+            regroup_wg(scalar, 1, 1)
             transpose_x(1)
-            regroup_wg(nc.vector.tensor_copy, 0, 0)
-            regroup_wg(nc.vector.tensor_copy, 1, 0)
+            copy_x(scalar, 1)
+            regroup_wg(vector, 0, 0)
+            regroup_wg(vector, 1, 0)
             quantise_wg(0, 0)
             quantise_wg(1, 0)
+            quantise_x(1)
             gate_matmul(0, 0)
             gate_matmul(0, 1)
-            gate_times_weighed_norm(0, 0)
-            quantise_x(1)
-            gate_times_weighed_norm(0, 1)
-            regroup_wg(nc.scalar.copy, 0, 3)
+            square_o(1, range(0, 2))
+            regroup_wg(scalar, 0, 3)
+            regroup_wg(scalar, 1, 3)
+            regroup_wg(vector, 0, 2)
+            stt(0, 0)
+            stt(0, 1)
+            regroup_wg(vector, 1, 2)
             transpose_x(2)
-            regroup_wg(nc.scalar.copy, 1, 3)
-            square_o(1)
-            regroup_wg(nc.vector.tensor_copy, 0, 2)
-            regroup_wg(nc.vector.tensor_copy, 1, 2)
+            copy_x(scalar, 2)
+            transpose_h(0, 0)
             quantise_wg(0, 1)
             quantise_wg(1, 1)
-            quantise_x(2)
             gate_matmul(0, 2)
             gate_matmul(0, 3)
-            gate_times_weighed_norm(0, 2)
-            gate_times_weighed_norm(0, 3)
             weigh_o(1)
+            stt(0, 2)
+            stt(0, 3)
+            square_o(1, range(2, HEADS))
+            invert_rms(1)
+            gate_matmul(1, 0)
+            quantise_x(2)
 
-        for step in range(1, T_TILES + 1):
-            transpose_h_words(step - 1)
-            copy_h_words(step - 1)
-            if step + 2 < T_TILES:
-                transpose_x(step + 2)
-            if step < T_TILES:
-                gate_matmul(step, 0)
-                gate_matmul(step, 1)
-            if step == 1:
-                for pair_of_heads in range(2):
-                    regroup_wo(nc.scalar.copy, 2 * pair_of_heads, 0)
-                    regroup_wo(nc.scalar.copy, 2 * pair_of_heads + 1, 0)
-                    quantise_wo(pair_of_heads, 0)
-            if step + 1 < T_TILES:
-                square_o(step + 1)
-            if step >= 2:
-                project_and_store(step - 2, 0)
-            if step < T_TILES:
-                gate_matmul(step, 2)
-                gate_matmul(step, 3)
-            if step > SECOND_HALF + 1:
-                while tiles_done[1] <= step - 3:
-                    project_and_store(tiles_done[1], 1)
-            if step + 2 < T_TILES:
-                quantise_x(step + 2)
-            if step < T_TILES:
-                quantise_h(step - 1)
+            for i in range(1, T_TILES):
+                first = {3: (0, 1)}.get(i, (i - 2,) if i > 3 else ())
+                second = {4: (0, 1, 2)}.get(i, (i - 2,) if i > 4 else ())
+                quarter = {1: (0, 0), 2: (1, 0), 3: (0, 1), 4: (1, 1)}.get(i)
+                if i + 2 < T_TILES:
+                    transpose_x(i + 2)
+                if i > 1:
+                    transpose_h(i - 1, 0)
+                transpose_h(i - 1, 1)
+                for tile in first:
+                    project(tile, 0)
+                if i == 1:
+                    gate_matmul(1, 1)
+                    gate_matmul(1, 2)
+                gate_matmul(i, 3)
+                if quarter is not None:
+                    pair_of_heads, half = quarter
+                    regroup_wo(scalar, 2 * pair_of_heads, half)
+                    if half == 0:
+                        regroup_wo(scalar, 2 * pair_of_heads + 1, half)
+                copy_h(i - 1, 0)
+                copy_h(i - 1, 1)
+                for tile in first:
+                    store(scalar, tile, 0)
+                if i + 2 < T_TILES:
+                    copy_x(scalar, i + 2)
+                if i + 1 < T_TILES:
+                    square_o(i + 1)
+                    invert_rms(i + 1)
                 for head in range(HEADS):
-                    gate_times_weighed_norm(step, head)
-            if step + 1 < T_TILES:
-                weigh_o(step + 1)
-            if step in (SECOND_HALF, SECOND_HALF + 1):
-                pair_of_heads = step - SECOND_HALF
-                regroup_wo(nc.scalar.copy, 2 * pair_of_heads, 1)
-                regroup_wo(nc.vector.tensor_copy, 2 * pair_of_heads + 1, 1)
-                quantise_wo(pair_of_heads, 1)
-        project_and_store(T_TILES - 2, 1)
-        finish_last_tile(T_TILES - 1)
+                    stt(i, head)
+                if quarter is not None:
+                    quantise_wo(*quarter)
+                quantise_h(i - 1)
+                if i + 1 < T_TILES:
+                    weigh_o(i + 1)
+                if i == 1:
+                    regroup_wo(vector, 1, 1)
+                    regroup_wo(vector, 3, 1)
+                if i + 2 < T_TILES:
+                    quantise_x(i + 2)
+                if i + 1 < T_TILES:
+                    for head in range(HEADS - 1):
+                        gate_matmul(i + 1, head)
+                for tile in second:
+                    project(tile, 1)
+                    store(scalar, tile, 1)
+            last = T_TILES - 1
+            transpose_h(last, 0)
+            transpose_h(last, 1)
+            copy_h(last, 0)
+            copy_h(last, 1)
+            for half in range(N_HALVES):
+                project(last - 1, half)
+                store(scalar, last - 1, half)
+            quantise_h(last, slice(0, 2))
+            quantise_h(last, slice(2, 4))
+            for pair_of_heads in range(2):
+                for half in range(N_HALVES):
+                    project(last, half, (pair_of_heads,))
+            store(vector, last, 0)
+            store(scalar, last, 1)

@@ -64,14 +64,13 @@ def tile_multiscaleretention_pc_kernel(tc, o_ret, x, Wg, gn_weight, Wo, out):
             cols = slice(DV * heads.start, DV * heads.stop)
             nc.sync.dma_start(out=o_raw[:, i, cols], in_=o_view[:, i, cols])
 
-        def load_wg(c, head_pair, parts=(slice(0, 2 * DV),)):
+        def load_wg(c, head_pair):
+            cols = slice(2 * DV * head_pair, 2 * DV * (head_pair + 1))
             wg_raw[(c, head_pair)] = w_raw.tile([P, PACK, 2 * DV], BF16, name="wg_raw", tag="w_raw")
-            for part in parts:
-                cols = slice(2 * DV * head_pair + part.start, 2 * DV * head_pair + part.stop)
-                nc.sync.dma_start(
-                    out=wg_raw[(c, head_pair)][:, :, part],
-                    in_=Wg[K_PASS * c : K_PASS * (c + 1), cols].rearrange("(p j) f -> p j f", j=PACK),
-                )
+            nc.sync.dma_start(
+                out=wg_raw[(c, head_pair)][:],
+                in_=Wg[K_PASS * c : K_PASS * (c + 1), cols].rearrange("(p j) f -> p j f", j=PACK),
+            )
 
         def load_wo(head, half):
             cols = slice(N_TILE * half, N_TILE * (half + 1))
@@ -85,7 +84,7 @@ def tile_multiscaleretention_pc_kernel(tc, o_ret, x, Wg, gn_weight, Wo, out):
         load_o(0, slice(0, 2))
         load_o(0, slice(2, HEADS))
         load_x(0)
-        load_wg(0, 0, (slice(DV, 2 * DV), slice(0, DV)))
+        load_wg(0, 0)
         load_wg(1, 0)
         load_x(1)
         load_o(1)
@@ -93,14 +92,19 @@ def tile_multiscaleretention_pc_kernel(tc, o_ret, x, Wg, gn_weight, Wo, out):
         load_wg(0, 1)
         load_wg(1, 1)
         load_o(2)
-        for head in range(HEADS):
-            load_wo(head, 0)
-        for i in range(3, 6):
-            load_x(i)
-            load_o(i)
-        for head in range(HEADS):
-            load_wo(head, 1)
-        for i in range(6, T_TILES):
+        load_wo(0, 0)
+        load_wo(1, 0)
+        load_x(3)
+        load_wo(2, 0)
+        load_o(3)
+        load_wo(3, 0)
+        load_wo(0, 1)
+        load_wo(3, 1)
+        load_x(4)
+        load_o(4)
+        load_wo(1, 1)
+        load_wo(2, 1)
+        for i in range(5, T_TILES):
             load_x(i)
             load_o(i)
 
@@ -337,7 +341,7 @@ def tile_multiscaleretention_pc_kernel(tc, o_ret, x, Wg, gn_weight, Wo, out):
             quantise_x(1)
             gate_matmul(0, 0)
             gate_matmul(0, 1)
-            square_o(1, range(0, 2))
+            square_o(1, range(0, 3))
             regroup_wg(scalar, 0, 3)
             regroup_wg(scalar, 1, 3)
             regroup_wg(vector, 0, 2)
@@ -354,7 +358,7 @@ def tile_multiscaleretention_pc_kernel(tc, o_ret, x, Wg, gn_weight, Wo, out):
             weigh_o(1)
             stt(0, 2)
             stt(0, 3)
-            square_o(1, range(2, HEADS))
+            square_o(1, range(3, HEADS))
             invert_rms(1)
             gate_matmul(1, 0)
             quantise_x(2)
@@ -362,42 +366,43 @@ def tile_multiscaleretention_pc_kernel(tc, o_ret, x, Wg, gn_weight, Wo, out):
             for i in range(1, T_TILES):
                 first = {3: (0, 1)}.get(i, (i - 2,) if i > 3 else ())
                 second = {4: (0, 1, 2)}.get(i, (i - 2,) if i > 4 else ())
-                quarter = {1: (0, 0), 2: (1, 0), 3: (0, 1), 4: (1, 1)}.get(i)
-                if i + 2 < T_TILES:
-                    transpose_x(i + 2)
                 if i > 1:
                     transpose_h(i - 1, 0)
                 transpose_h(i - 1, 1)
+                if i + 2 < T_TILES:
+                    transpose_x(i + 2)
                 for tile in first:
                     project(tile, 0)
                 if i == 1:
                     gate_matmul(1, 1)
                     gate_matmul(1, 2)
                 gate_matmul(i, 3)
-                if quarter is not None:
-                    pair_of_heads, half = quarter
-                    regroup_wo(scalar, 2 * pair_of_heads, half)
-                    if half == 0:
-                        regroup_wo(scalar, 2 * pair_of_heads + 1, half)
+                for head, half in {1: ((0, 0), (1, 0)), 2: ((2, 0), (3, 0)), 3: ((1, 1),), 4: ((2, 1),)}.get(i, ()):
+                    regroup_wo(scalar, head, half)
                 copy_h(i - 1, 0)
                 copy_h(i - 1, 1)
-                for tile in first:
-                    store(scalar, tile, 0)
-                if i + 2 < T_TILES:
-                    copy_x(scalar, i + 2)
                 if i + 1 < T_TILES:
                     square_o(i + 1)
+                if i + 2 < T_TILES:
+                    copy_x(scalar, i + 2)
+                for tile in first:
+                    store(scalar, tile, 0)
+                if i + 1 < T_TILES:
                     invert_rms(i + 1)
                 for head in range(HEADS):
                     stt(i, head)
-                if quarter is not None:
-                    quantise_wo(*quarter)
+                if i == 2:
+                    quantise_wo(0, 0)
+                    regroup_wo(vector, 0, 1)
+                    quantise_wo(1, 0)
+                if i == 3:
+                    quantise_wo(0, 1)
+                    regroup_wo(vector, 3, 1)
+                if i == 4:
+                    quantise_wo(1, 1)
                 quantise_h(i - 1)
                 if i + 1 < T_TILES:
                     weigh_o(i + 1)
-                if i == 1:
-                    regroup_wo(vector, 1, 1)
-                    regroup_wo(vector, 3, 1)
                 if i + 2 < T_TILES:
                     quantise_x(i + 2)
                 if i + 1 < T_TILES:

@@ -341,7 +341,7 @@ def tile_multiscaleretention_pc_kernel(tc, o_ret, x, Wg, gn_weight, Wo, out):
             quantise_x(1)
             gate_matmul(0, 0)
             gate_matmul(0, 1)
-            square_o(1, range(0, 3))
+            square_o(1)
             regroup_wg(scalar, 0, 3)
             regroup_wg(scalar, 1, 3)
             regroup_wg(vector, 0, 2)
@@ -358,53 +358,52 @@ def tile_multiscaleretention_pc_kernel(tc, o_ret, x, Wg, gn_weight, Wo, out):
             weigh_o(1)
             stt(0, 2)
             stt(0, 3)
-            square_o(1, range(3, HEADS))
             invert_rms(1)
             gate_matmul(1, 0)
             quantise_x(2)
 
             for i in range(1, T_TILES):
+                coming = {4: (6, 7)}.get(i, (i + 2,) if i < 4 else ())
                 first = {3: (0, 1)}.get(i, (i - 2,) if i > 3 else ())
                 second = {4: (0, 1, 2)}.get(i, (i - 2,) if i > 4 else ())
                 if i > 1:
                     transpose_h(i - 1, 0)
                 transpose_h(i - 1, 1)
-                if i + 2 < T_TILES:
-                    transpose_x(i + 2)
                 for tile in first:
                     project(tile, 0)
                 if i == 1:
                     gate_matmul(1, 1)
                     gate_matmul(1, 2)
                 gate_matmul(i, 3)
+                for tile in coming:
+                    transpose_x(tile)
                 for head, half in {1: ((0, 0), (1, 0)), 2: ((2, 0), (3, 0)), 3: ((1, 1),), 4: ((2, 1),)}.get(i, ()):
                     regroup_wo(scalar, head, half)
                 copy_h(i - 1, 0)
                 copy_h(i - 1, 1)
-                if i + 1 < T_TILES:
-                    square_o(i + 1)
-                if i + 2 < T_TILES:
-                    copy_x(scalar, i + 2)
                 for tile in first:
                     store(scalar, tile, 0)
+                if i + 1 < T_TILES:
+                    square_o(i + 1)
+                for tile in coming:
+                    copy_x(scalar, tile)
                 if i + 1 < T_TILES:
                     invert_rms(i + 1)
                 for head in range(HEADS):
                     stt(i, head)
                 if i == 2:
                     quantise_wo(0, 0)
-                    regroup_wo(vector, 0, 1)
                     quantise_wo(1, 0)
-                if i == 3:
-                    quantise_wo(0, 1)
                     regroup_wo(vector, 3, 1)
+                    regroup_wo(vector, 0, 1)
                 if i == 4:
+                    quantise_wo(0, 1)
                     quantise_wo(1, 1)
                 quantise_h(i - 1)
                 if i + 1 < T_TILES:
                     weigh_o(i + 1)
-                if i + 2 < T_TILES:
-                    quantise_x(i + 2)
+                for tile in coming:
+                    quantise_x(tile)
                 if i + 1 < T_TILES:
                     for head in range(HEADS - 1):
                         gate_matmul(i + 1, head)

import concourse.mybir as mybir
from concourse.masks import make_identity

FP8X4 = mybir.dt.float8_e4m3fn_x4
BF16 = mybir.dt.bfloat16
F32 = mybir.dt.float32
U32 = mybir.dt.uint32
U8 = mybir.dt.uint8
ACT = mybir.ActivationFunctionType
ALU = mybir.AluOpType

P = 128
PACK = 4
K_PASS = P * PACK
T = 1024
E = 1024
HEADS = 4
DV = 512
F = HEADS * DV
N_OUT = 1024
N_TILE = 512
T_TILES = T // P
E_PASSES = E // K_PASS
N_HALVES = N_OUT // N_TILE
EPS = 1e-5
OG_TILES = 2

FLOPS = 2 * T * E * F + 2 * T * F * N_OUT


def tile_multiscaleretention_pc_kernel(tc, o_ret, x, Wg, gn_weight, Wo, out):
    nc = tc.nc
    x_view = x.flatten_outer_dims().rearrange("(p i) e -> p i e", i=T_TILES)
    o_view = o_ret.rearrange("b t h d -> (b t) (h d)").rearrange("(p i) f -> p i f", i=T_TILES)
    out_view = out.flatten_outer_dims().rearrange("(p i) n -> p i n", i=T_TILES)

    with tc.tile_pool(name="keep", bufs=1) as keep, tc.tile_pool(name="w_stage", bufs=3) as w_stage, tc.tile_pool(
        name="w_raw", bufs=6
    ) as w_raw, tc.tile_pool(name="x_pool", bufs=4) as x_pool, tc.tile_pool(
        name="og_pool", bufs=OG_TILES
    ) as og_pool, tc.tile_pool(name="hb_pool", bufs=2 * HEADS) as hb_pool, tc.tile_pool(name="pair", bufs=2) as pair, tc.tile_pool(name="result_pool", bufs=6) as result_pool, tc.psum_pool(name="psum_g", bufs=3) as psum_g, tc.psum_pool(
        name="psum_t", bufs=5
    ) as psum_t:
        gn_cols = keep.tile([P, PACK], BF16)
        ident = keep.tile([P, P], F32)
        make_identity(nc, ident[:])
        ident_bf16 = keep.tile([P, P], BF16)
        make_identity(nc, ident_bf16[:])
        eps_col = keep.tile([P, 1], F32)
        nc.vector.memset(eps_col[:], EPS)
        warm = keep.tile([P, 1], F32)
        nc.scalar.activation(out=warm[:], in_=eps_col[:], func=ACT.Abs_reciprocal_sqrt)

        x_raw = {}
        wg_raw = {}
        o_raw = keep.tile([P, T_TILES, F], BF16)
        wo_raw = {}

        def load_x(i):
            x_raw[i] = x_pool.tile([P, E], BF16, name="x_raw", tag="x_raw")
            nc.sync.dma_start(out=x_raw[i][:], in_=x_view[:, i, :])

        def load_o(i, heads=slice(0, HEADS)):
            cols = slice(DV * heads.start, DV * heads.stop)
            nc.sync.dma_start(out=o_raw[:, i, cols], in_=o_view[:, i, cols])

        def load_wg(c, head_pair):
            cols = slice(2 * DV * head_pair, 2 * DV * (head_pair + 1))
            wg_raw[(c, head_pair)] = w_raw.tile([P, PACK, 2 * DV], BF16, name="wg_raw", tag="w_raw")
            nc.sync.dma_start(
                out=wg_raw[(c, head_pair)][:],
                in_=Wg[K_PASS * c : K_PASS * (c + 1), cols].rearrange("(p j) f -> p j f", j=PACK),
            )

        def load_wo(head, half):
            cols = slice(N_TILE * half, N_TILE * (half + 1))
            wo_raw[(head, half)] = w_raw.tile([P, PACK, N_TILE], BF16, name="wo_raw", tag="w_raw")
            nc.sync.dma_start(
                out=wo_raw[(head, half)][:],
                in_=Wo[K_PASS * head : K_PASS * (head + 1), cols].rearrange("(p j) n -> p j n", j=PACK),
            )

        nc.sync.dma_start(out=gn_cols[:], in_=gn_weight.rearrange("(p j) -> p j", j=PACK))
        load_o(0, slice(0, 2))
        load_o(0, slice(2, HEADS))
        load_x(0)
        load_wg(0, 0)
        load_wg(1, 0)
        load_x(1)
        load_o(1)
        load_x(2)
        load_wg(0, 1)
        load_wg(1, 1)
        load_o(2)
        load_wo(0, 0)
        load_wo(1, 0)
        load_x(3)
        load_wo(2, 0)
        load_o(3)
        load_wo(3, 0)
        load_wo(0, 1)
        load_wo(3, 1)
        load_x(4)
        load_o(4)
        load_wo(1, 1)
        load_wo(2, 1)
        for i in range(5, T_TILES):
            load_x(i)
            load_o(i)

        def in_word_order(features):
            return features.rearrange("t (p u e) -> t u p e", u=2, e=2)

        gn_all = keep.tile([P, 2, P, 2], F32)

        def spread_gn():
            gn_bank = psum_t.tile([P, PACK, P], F32, tag="t")
            for j in range(PACK):
                nc.tensor.matmul(
                    out=gn_bank[:, j, :],
                    lhsT=gn_cols[:, j : j + 1].to_broadcast([P, P]),
                    rhs=ident_bf16[:],
                    start=True,
                    stop=True,
                )
            nc.vector.tensor_copy(out=gn_all[:], in_=gn_bank[:].rearrange("t (u e) p -> t u p e", e=2))

        x_codes = keep.tile([P, T_TILES, E_PASSES, P], U32, align_bytes=256)
        x_scales = keep.tile([P, T_TILES, E_PASSES, P], U8, align_bytes=256)
        x_grouped = {}
        xt_banks = {}
        ssq = {}
        rinv = {}

        def transpose_x(i):
            xt = psum_t.tile([P, PACK, P], F32, tag="t")
            x_words = x_raw[i][:].bitcast(F32)
            for c in range(E_PASSES):
                for u in range(2):
                    nc.tensor.transpose(
                        xt[:, 2 * c + u, :], x_words[:, 2 * P * c + u : 2 * P * (c + 1) : 2], ident[:]
                    )
            xt_banks[i] = xt

        def copy_x(copy, i):
            grouped = pair.tile([P, E_PASSES, P, PACK], BF16, align_bytes=64, tag="x_grouped", name="x_grouped")
            copy(out=grouped[:].bitcast(F32), in_=xt_banks[i][:].rearrange("p (c u) t -> p c t u", u=2))
            x_grouped[i] = grouped

        def square_o(i, heads=range(HEADS)):
            if i not in ssq:
                ssq[i] = keep.tile([P, HEADS], F32, name="ssq%d" % i)
            for head in heads:
                squares = pair.tile([P, DV], BF16, tag="squares")
                nc.scalar.activation(
                    out=squares[:],
                    in_=o_raw[:, i, DV * head : DV * (head + 1)],
                    func=ACT.Square,
                    accum_out=ssq[i][:, head : head + 1],
                )

        def invert_rms(i):
            rinv[i] = keep.tile([P, HEADS], F32, name="rinv%d" % i)
            nc.scalar.activation(
                out=rinv[i][:], in_=ssq[i][:], func=ACT.Abs_reciprocal_sqrt, scale=1.0 / DV, bias=eps_col[:]
            )

        def quantise_x(i):
            nc.vector.quantize_mx(
                out=x_codes[:, i, :, :].rearrange("p c t -> p (c t)").bitcast(FP8X4),
                scales=x_scales[:, i, :, :].rearrange("p c t -> p (c t)"),
                in_=x_grouped[i][:].rearrange("p c t j -> p (c t j)"),
            )

        wg_codes = keep.tile([P, E_PASSES, F], U32, align_bytes=256)
        wg_scales = keep.tile([P, E_PASSES, F], U8, align_bytes=256)
        wo_codes = keep.tile([P, N_HALVES, HEADS, N_TILE], U32, align_bytes=256)
        wo_scales = keep.tile([P, N_HALVES, HEADS, N_TILE], U8, align_bytes=256)

        def new_weights():
            return w_stage.tile([P, 2, N_TILE, PACK], BF16, align_bytes=64, name="w_grouped", tag="w_grouped")

        def regroup(copy, grouped, rows):
            copy(
                out=grouped.rearrange("p (c i) j -> p c j i", i=4),
                in_=rows.rearrange("p j (c i) -> p c j i", i=4),
            )

        def regroup_in_word_order(copy, grouped, rows):
            copy(
                out=grouped.rearrange("p (u c e) j -> p c j u e", u=2, e=2),
                in_=rows.rearrange("p j (c u e) -> p c j u e", u=2, e=2),
            )

        def quantise_weights(grouped, codes, scales):
            nc.vector.quantize_mx(
                out=codes.bitcast(FP8X4), scales=scales, in_=grouped[:].rearrange("p h w j -> p (h w j)")
            )

        wg_grouped = {}

        def regroup_wg(copy, c, head):
            pair_of_heads, odd = divmod(head, 2)
            if (c, pair_of_heads) not in wg_grouped:
                wg_grouped[(c, pair_of_heads)] = new_weights()
            rows = wg_raw[(c, pair_of_heads)][:, :, DV * odd : DV * (odd + 1)]
            regroup_in_word_order(copy, wg_grouped[(c, pair_of_heads)][:, odd, :, :], rows)

        def quantise_wg(c, pair_of_heads):
            cols = slice(2 * DV * pair_of_heads, 2 * DV * (pair_of_heads + 1))
            quantise_weights(wg_grouped[(c, pair_of_heads)], wg_codes[:, c, cols], wg_scales[:, c, cols])

        wo_grouped = {}

        def regroup_wo(copy, head, half):
            pair_of_heads, odd = divmod(head, 2)
            if (pair_of_heads, half) not in wo_grouped:
                wo_grouped[(pair_of_heads, half)] = new_weights()
            regroup(copy, wo_grouped[(pair_of_heads, half)][:, odd, :, :], wo_raw[(head, half)][:])

        def quantise_wo(pair_of_heads, half):
            heads = slice(2 * pair_of_heads, 2 * pair_of_heads + 2)
            quantise_weights(
                wo_grouped[(pair_of_heads, half)],
                wo_codes[:, half, heads, :].rearrange("p h n -> p (h n)"),
                wo_scales[:, half, heads, :].rearrange("p h n -> p (h n)"),
            )

        h_codes = keep.tile([P, T_TILES, HEADS, P], U32, align_bytes=256)
        h_scales = keep.tile([P, T_TILES, HEADS, P], U8, align_bytes=256)
        g_banks = {}
        h0_tiles = {}
        og_tiles = {}
        h_grouped_tiles = {}
        ht_banks = {}

        def weigh_o(i, heads=slice(0, HEADS)):
            if i not in og_tiles:
                og_tiles[i] = og_pool.tile([P, 2, HEADS, P, 2], F32, name="og", tag="og")
            o_words = o_raw[:, i, :].rearrange("t (h p u e) -> t u h p e", h=HEADS, u=2, e=2)
            nc.vector.tensor_tensor(
                out=og_tiles[i][:, :, heads, :, :],
                in0=o_words[:, :, heads, :, :],
                in1=gn_all[:].unsqueeze(2).to_broadcast([P, 2, heads.stop - heads.start, P, 2]),
                op=ALU.mult,
            )

        def gate_matmul(i, head):
            cols = slice(DV * head, DV * (head + 1))
            g = psum_g.tile([P, DV], F32, tag="g")
            for c in range(E_PASSES):
                nc.tensor.matmul_mx(
                    out=g[:],
                    lhsT=x_codes[:, i, c, :].bitcast(FP8X4),
                    lhsT_scale=x_scales[:, i, c, :],
                    rhs=wg_codes[:, c, cols].bitcast(FP8X4),
                    rhs_scale=wg_scales[:, c, cols],
                    start=(c == 0),
                    stop=(c == E_PASSES - 1),
                )
            g_banks[(i, head)] = g

        def gate_times_weighed_norm(i, head):
            h0 = hb_pool.tile([P, DV], BF16, tag="hb")
            nc.vector.scalar_tensor_tensor(
                out=h0[:].rearrange("t (u w) -> t u w", u=2),
                in0=g_banks[(i, head)][:].rearrange("t (u w) -> t u w", u=2),
                scalar=rinv[i][:, head : head + 1],
                in1=og_tiles[i][:, :, head, :, :].rearrange("t u p e -> t u (p e)"),
                op0=ALU.mult,
                op1=ALU.mult,
            )
            h0_tiles[(i, head)] = h0

        def transpose_h(i, pair_of_heads):
            ht = psum_t.tile([P, PACK, P], F32, tag="t", name="ht")
            for hu in range(PACK):
                words = h0_tiles[(i, 2 * pair_of_heads + hu // 2)][:].bitcast(F32)
                u = hu % 2
                nc.tensor.transpose(ht[:, hu, :], words[:, P * u : P * (u + 1)], ident[:])
            ht_banks[(i, pair_of_heads)] = ht

        def copy_h(i, pair_of_heads):
            if i not in h_grouped_tiles:
                h_grouped_tiles[i] = pair.tile(
                    [P, HEADS, P, PACK], BF16, align_bytes=64, tag="h_grouped", name="h_grouped"
                )
            nc.scalar.copy(
                out=h_grouped_tiles[i][:, 2 * pair_of_heads : 2 * pair_of_heads + 2, :, :].bitcast(F32),
                in_=ht_banks[(i, pair_of_heads)][:].rearrange("p (h u) t -> p h t u", u=2),
            )

        def quantise_h(i, heads=slice(0, HEADS)):
            nc.vector.quantize_mx(
                out=h_codes[:, i, heads, :].rearrange("p h t -> p (h t)").bitcast(FP8X4),
                scales=h_scales[:, i, heads, :].rearrange("p h t -> p (h t)"),
                in_=h_grouped_tiles[i][:, heads, :, :].rearrange("p h t j -> p (h t j)"),
            )

        acc_banks = {}

        def project(i, half, pairs=(0, 1)):
            if (i, half) not in acc_banks:
                acc_banks[(i, half)] = psum_t.tile([P, N_TILE], F32, name="acc", tag="t")
            for pair_of_heads in pairs:
                for head in (2 * pair_of_heads, 2 * pair_of_heads + 1):
                    nc.tensor.matmul_mx(
                        out=acc_banks[(i, half)][:],
                        lhsT=h_codes[:, i, head, :].bitcast(FP8X4),
                        lhsT_scale=h_scales[:, i, head, :],
                        rhs=wo_codes[:, half, head, :].bitcast(FP8X4),
                        rhs_scale=wo_scales[:, half, head, :],
                        start=(head == 0),
                        stop=(head == HEADS - 1),
                    )

        def store(copy, i, half):
            result = result_pool.tile([P, N_TILE], F32, name="result", tag="result")
            copy(out=result[:], in_=acc_banks[(i, half)][:])
            nc.sync.dma_start(out=out_view[:, i, N_TILE * half : N_TILE * (half + 1)], in_=result[:])

        vector, scalar = nc.vector.tensor_copy, nc.scalar.copy
        stt = gate_times_weighed_norm
        with tc.manual_schedule(engines={mybir.EngineType.PE, mybir.EngineType.DVE, mybir.EngineType.Activation}):
            spread_gn()
            transpose_x(0)
            square_o(0)
            invert_rms(0)
            weigh_o(0, slice(0, 2))
            weigh_o(0, slice(2, HEADS))
            copy_x(vector, 0)
            quantise_x(0)
            regroup_wg(scalar, 0, 1)
            regroup_wg(scalar, 1, 1)
            transpose_x(1)
            copy_x(scalar, 1)
            regroup_wg(vector, 0, 0)
            regroup_wg(vector, 1, 0)
            quantise_wg(0, 0)
            quantise_wg(1, 0)
            quantise_x(1)
            gate_matmul(0, 0)
            gate_matmul(0, 1)
            square_o(1)
            regroup_wg(scalar, 0, 3)
            regroup_wg(scalar, 1, 3)
            regroup_wg(vector, 0, 2)
            stt(0, 0)
            stt(0, 1)
            regroup_wg(vector, 1, 2)
            transpose_x(2)
            copy_x(scalar, 2)
            transpose_h(0, 0)
            quantise_wg(0, 1)
            quantise_wg(1, 1)
            gate_matmul(0, 2)
            gate_matmul(0, 3)
            weigh_o(1)
            stt(0, 2)
            stt(0, 3)
            invert_rms(1)
            gate_matmul(1, 0)
            quantise_x(2)

            for i in range(1, T_TILES):
                coming = {4: (6, 7)}.get(i, (i + 2,) if i < 4 else ())
                first = {3: (0, 1)}.get(i, (i - 2,) if i > 3 else ())
                second = {4: (0, 1, 2)}.get(i, (i - 2,) if i > 4 else ())
                if i > 1:
                    transpose_h(i - 1, 0)
                transpose_h(i - 1, 1)
                for tile in first:
                    project(tile, 0)
                if i == 1:
                    gate_matmul(1, 1)
                    gate_matmul(1, 2)
                gate_matmul(i, 3)
                for tile in coming:
                    transpose_x(tile)
                for head, half in {1: ((0, 0), (1, 0)), 2: ((2, 0), (3, 0)), 3: ((1, 1),), 4: ((2, 1),)}.get(i, ()):
                    regroup_wo(scalar, head, half)
                copy_h(i - 1, 0)
                copy_h(i - 1, 1)
                for tile in first:
                    store(scalar, tile, 0)
                if i + 1 < T_TILES:
                    square_o(i + 1)
                for tile in coming:
                    copy_x(scalar, tile)
                if i + 1 < T_TILES:
                    invert_rms(i + 1)
                for head in range(HEADS):
                    stt(i, head)
                if i == 2:
                    quantise_wo(0, 0)
                    quantise_wo(1, 0)
                    regroup_wo(vector, 3, 1)
                    regroup_wo(vector, 0, 1)
                if i == 4:
                    quantise_wo(0, 1)
                    quantise_wo(1, 1)
                quantise_h(i - 1)
                if i + 1 < T_TILES:
                    weigh_o(i + 1)
                for tile in coming:
                    quantise_x(tile)
                if i + 1 < T_TILES:
                    for head in range(HEADS - 1):
                        gate_matmul(i + 1, head)
                for tile in second:
                    project(tile, 1)
                    store(scalar, tile, 1)
            last = T_TILES - 1
            transpose_h(last, 0)
            transpose_h(last, 1)
            copy_h(last, 0)
            copy_h(last, 1)
            for half in range(N_HALVES):
                project(last - 1, half)
                store(scalar, last - 1, half)
            quantise_h(last, slice(0, 2))
            quantise_h(last, slice(2, 4))
            for pair_of_heads in range(2):
                for half in range(N_HALVES):
                    project(last, half, (pair_of_heads,))
            store(vector, last, 0)
            store(scalar, last, 1)
